import numpy as np
import ml_dtypes


def mxq(x, axis, fmt="e4m3"):
    dtype, down = {"e4m3": (ml_dtypes.float8_e4m3fn, 7), "e5m2": (ml_dtypes.float8_e5m2, 14)}[fmt]
    v = np.moveaxis(np.asarray(x, np.float32).astype(ml_dtypes.bfloat16).astype(np.float64), axis, -1)
    blocks = v.reshape(v.shape[:-1] + (-1, 32))
    amax = np.abs(blocks).max(-1, keepdims=True)
    byte = np.maximum(np.where(amax > 0, np.frexp(amax)[1] - 1 + 127, 0) - down, 1)
    scale = np.exp2(byte - 127.0)
    codes = (blocks / scale).astype(np.float32).astype(dtype).astype(np.float64)
    return np.moveaxis((codes * scale).reshape(v.shape), -1, axis)


WIDE = False


def mx_kscale(k):
    if not WIDE:
        return np.ones(k)
    levels = np.array([10, -10, 5, -5, 0])
    a = np.random.permutation(np.resize(levels, k // 512 * 4)).reshape(k // 512, 4)
    idx = np.arange(k)
    return np.exp2(a[idx // 512, idx % 128 // 32])


BF16 = ml_dtypes.bfloat16


def bf(x):
    return np.asarray(x, np.float32).astype(BF16)


def f64(x):
    return np.asarray(x).astype(np.float64)


B, N, E, L, A, H1, H2, G = 256, 8, 8, 384, 128, 1024, 1024, 8
D = L + A
EPS = 1e-5


def mish(v):
    return v * np.tanh(np.log(1.0 + np.exp(v)))


def layer_norm(v, gamma, beta):
    mu = v.mean(-1, keepdims=True)
    var = v.var(-1, keepdims=True)
    return (v - mu) / np.sqrt(var + EPS) * gamma + beta


def setup_inputs():
    s = mx_kscale(D)
    r = np.random.standard_normal
    return {"tokens": bf(r((B, N, D)) * s),
            "logits": bf(r((B, N, E))),
            "W1": bf(r((E, D, H1)) / np.sqrt(D) / s[:, None]),
            "b1": bf(0.1 * r((E, H1))),
            "g1": bf(1.0 + 0.1 * r((E, H1))),
            "be1": bf(0.1 * r((E, H1)))}


def reference(tokens, logits, W1, b1, g1, be1):
    tok, lg = f64(tokens), f64(logits)
    ex = np.exp(lg - lg.max(1, keepdims=True))
    disp = ex / ex.sum(1, keepdims=True)
    slot = sum(disp[:, n, :].T[:, :, None] * tok[None, :, n, :] for n in range(N))
    h = (mxq(slot, 2, "e4m3") @ mxq(f64(W1), 1, "e4m3")) + f64(b1)[:, None, :]
    h = mish(layer_norm(h, f64(g1)[:, None, :], f64(be1)[:, None, :]))
    return h.transpose(1, 0, 2)

@@ -1,0 +1,412 @@
+from contextlib import ExitStack
+
+import concourse.mybir as mybir
+from concourse.masks import make_identity
+
+F32 = mybir.dt.float32
+BF16 = mybir.dt.bfloat16
+U32 = mybir.dt.uint32
+U8 = mybir.dt.uint8
+FP8X4 = mybir.dt.float8_e4m3fn_x4
+ALU = mybir.AluOpType
+ACT = mybir.ActivationFunctionType
+AX = mybir.AxisListType
+
+P = 128
+B, NA, E, D, H = 256, 8, 8, 512, 1024
+G = 16
+GB = 16
+PACK = 4
+EPS = 1e-5
+EP = 6
+HV = (512, 512, 256, 256, 1024, 1024, 1024, 1024)
+ACT_STEP = {0: (0, 512), 1: (0, 768), 2: (1, 512), 3: (1, 768), 6: (2, 256), 7: (2, 512), 8: (2, 768),
+            10: (3, 256), 11: (3, 512), 12: (3, 768)}
+F_ON_POOL = (0, 1, 2, 3, 4, 5)
+FILL1, FILL2, FILL3 = 2.0, 2.0, 2.5
+
+FLOPS = 2 * E * B * D * H + 2 * B * NA * E * D
+
+
+def tile_softmoedynamics_pa_kernel(tc, tokens, logits, W1, b1, g1, be1, out):
+    nc = tc.nc
+    with ExitStack() as ctx:
+        cst = ctx.enter_context(tc.tile_pool(name="cst", bufs=1))
+        xp = ctx.enter_context(tc.tile_pool(name="xp", bufs=6))
+        up = ctx.enter_context(tc.tile_pool(name="up", bufs=6))
+        tnp = ctx.enter_context(tc.tile_pool(name="tnp", bufs=1))
+        wrp = ctx.enter_context(tc.tile_pool(name="wrp", bufs=3))
+        wgp = ctx.enter_context(tc.tile_pool(name="wgp", bufs=2))
+        wcp = ctx.enter_context(tc.tile_pool(name="wcp", bufs=5))
+        bbp = ctx.enter_context(tc.tile_pool(name="bbp", bufs=3))
+        acp = ctx.enter_context(tc.tile_pool(name="acp", bufs=1))
+        stp = ctx.enter_context(tc.tile_pool(name="stp", bufs=8))
+        psH = ctx.enter_context(tc.psum_pool(name="psH", bufs=4))
+        psG = ctx.enter_context(tc.psum_pool(name="psG", bufs=2))
+        ctx.enter_context(tc.manual_schedule())
+
+        ident = cst.tile([P, P], F32, name="ident")
+        make_identity(nc, ident[:])
+        identb = cst.tile([P, P], BF16, name="identb")
+        make_identity(nc, identb[:])
+        mhalf = cst.tile([P, 2], F32, name="mhalf")
+        nc.gpsimd.memset(mhalf[:], -0.5)
+
+        lg_raw = cst.tile([P, G, 16], BF16, name="lg_raw")
+        nc.sync.dma_start(out=lg_raw[:, :, 0:E], in_=logits.rearrange("(g b) n e -> (b n) g e", b=GB))
+        rows = cst.tile([P, P], BF16, name="rows")
+        nc.sync.dma_start(out=rows[0:64, :], in_=g1.rearrange("e (c q) -> (e c) q", q=P))
+        nc.sync.dma_start(out=rows[64:128, :], in_=be1.rearrange("e (c q) -> (e c) q", q=P))
+        lgn = cst.tile([P, 2, NA * E], BF16, name="lgn")
+        nc.sync.dma_start(out=lgn[:], in_=logits.rearrange("(t b) n e -> b t (n e)", b=P))
+        tok_view = tokens.rearrange("(g b) n d -> (b n) g d", b=GB)
+        trs = []
+        for q in range(4):
+            tr = up.tile([P, 4, D], BF16, tag="u", name="tr%d" % q)
+            nc.sync.dma_start(out=tr[:], in_=tok_view[:, 4 * q:4 * q + 4, :])
+            trs.append(tr)
+
+        wrs, wgs, wcs, wss, bbs, tns = {}, {}, {}, {}, {}, {}
+
+        def wload(e):
+            wr = wrp.tile([P, PACK, H], BF16, tag="wr", name="wr%d" % e)
+            nc.sync.dma_start(out=wr[:], in_=W1[e].rearrange("(j p) h -> p j h", p=P))
+            wrs[e] = wr
+
+        def bload(e, eng):
+            bb = bbp.tile([P, H], BF16, tag="bb", name="bb%d" % e)
+            eng.dma_start(out=bb[:], in_=b1[e].partition_broadcast(P))
+            bbs[e] = bb
+
+        def tnload(t):
+            tn = tnp.tile([P, NA, D], BF16, tag="tn", name="tn%d" % t)
+            nc.sync.dma_start(out=tn[:], in_=tokens[P * t:P * t + P])
+            tns[t] = tn
+
+        wload(0)
+        wload(1)
+        tnload(0)
+        wload(2)
+        for e in range(3):
+            bload(e, nc.gpsimd)
+
+        mask = cst.tile([P, GB], F32, name="mask")
+        nc.vector.tensor_reduce(out=mask[:], in_=ident[:].rearrange("p (b n) -> p b n", n=NA), axis=AX.X, op=ALU.add)
+        lgf = cst.tile([P, G, E], F32, name="lgf")
+        nc.vector.tensor_copy(out=lgf[:], in_=lg_raw[:, :, 0:E])
+        psT = psH.tile([P, GB, NA], F32, tag="ph", name="psT")
+        nc.tensor.transpose(psT[:].rearrange("p b n -> p (b n)"), lgf[:].rearrange("p g e -> p (g e)"), ident[:])
+        psR = psH.tile([P, P], BF16, tag="ph", name="psR")
+        nc.tensor.transpose(psR[:], rows[:], identb[:])
+        mx = cst.tile([P, GB], F32, name="mx")
+        nc.vector.tensor_reduce(out=mx[:], in_=psT[:], axis=AX.X, op=ALU.max)
+        sh = cst.tile([P, GB, NA], F32, name="sh")
+        nc.vector.tensor_tensor(out=sh[:], in0=psT[:], in1=mx[:].unsqueeze(2).to_broadcast([P, GB, NA]), op=ALU.subtract)
+        nc.scalar.activation(out=sh[:], in_=sh[:], func=ACT.Exp)
+
+        tfs = []
+
+        def cast(q):
+            tf = xp.tile([P, 4, D], F32, tag="x", name="tf%d" % q)
+            nc.vector.tensor_copy(out=tf[:], in_=trs[q][:])
+            tfs.append(tf)
+
+        cast(0)
+        sm = cst.tile([P, GB], F32, name="sm")
+        nc.vector.tensor_reduce(out=sm[:], in_=sh[:], axis=AX.X, op=ALU.add)
+        rs = cst.tile([P, GB], F32, name="rs")
+        nc.vector.reciprocal(out=rs[:], in_=sm[:])
+        nc.vector.tensor_tensor(out=sh[:], in0=sh[:], in1=rs[:].unsqueeze(2).to_broadcast([P, GB, NA]), op=ALU.mult)
+        psD = psH.tile([P, G, E], F32, tag="ph", name="psD")
+        nc.tensor.transpose(psD[:].rearrange("p g e -> p (g e)"), sh[:].rearrange("p b n -> p (b n)"), ident[:])
+        gcol = cst.tile([P, P], BF16, name="gcol")
+        nc.vector.tensor_copy(out=gcol[:], in_=psR[:])
+        cast(1)
+        dblk = cst.tile([P, G, EP, GB], F32, name="dblk")
+        for g0 in (0, 8):
+            nc.vector.tensor_tensor(
+                out=dblk[:, g0:g0 + 8, :, :],
+                in0=psD[:, g0:g0 + 8, 0:EP].unsqueeze(3).to_broadcast([P, 8, EP, GB]),
+                in1=mask[:].unsqueeze(1).unsqueeze(1).to_broadcast([P, 8, EP, GB]),
+                op=ALU.mult,
+            )
+        cast(2)
+        cast(3)
+
+        NV = E - EP
+        dn = cst.tile([P, 2, NV, NA], F32, name="dn")
+        dnv = dn[:].rearrange("b t e n -> b (t e) n")
+        nc.vector.tensor_copy(out=dn[:], in_=lgn[:].rearrange("b t (n e) -> b t e n", e=E)[:, :, EP:E, :])
+        mxn = cst.tile([P, 2 * NV], F32, name="mxn")
+        nc.vector.tensor_reduce(out=mxn[:], in_=dnv, axis=AX.X, op=ALU.max)
+        nc.vector.tensor_tensor(out=dnv, in0=dnv, in1=mxn[:].unsqueeze(2).to_broadcast([P, 2 * NV, NA]), op=ALU.subtract)
+        nc.scalar.activation(out=dnv, in_=dnv, func=ACT.Exp)
+        smn = cst.tile([P, 2 * NV], F32, name="smn")
+        nc.vector.tensor_reduce(out=smn[:], in_=dnv, axis=AX.X, op=ALU.add)
+        rsn = cst.tile([P, 2 * NV], F32, name="rsn")
+        nc.vector.reciprocal(out=rsn[:], in_=smn[:])
+        nc.vector.tensor_tensor(out=dnv, in0=dnv, in1=rsn[:].unsqueeze(2).to_broadcast([P, 2 * NV, NA]), op=ALU.mult)
+
+        pgs, pbs = {}, {}
+
+        def peb(e):
+            pg = psG.tile([P, H], BF16, tag="pg", name="pg%d" % e)
+            pb = psG.tile([P, H], BF16, tag="pb", name="pb%d" % e)
+            for w, dst in ((0, pg), (1, pb)):
+                for c in range(8):
+                    col = 64 * w + 8 * e + c
+                    nc.tensor.transpose(dst[:, P * c:P * c + P], gcol[:, col:col + 1].to_broadcast([P, P]), identb[:])
+            pgs[e] = pg
+            pbs[e] = pb
+
+        peb(0)
+        peb(1)
+
+        def regroup(copy_fn, e, c0, c1):
+            if e not in wgs:
+                wgs[e] = wgp.tile([P, H, PACK], BF16, tag="wg", name="wg%d" % e, align_bytes=64)
+            copy_fn(
+                out=wgs[e][:, c0:c1, :].rearrange("p (c i) t -> p c t i", i=4),
+                in_=wrs[e][:, :, c0:c1].rearrange("p t (c i) -> p c t i", i=4),
+            )
+
+        def wquant(e):
+            wcs[e] = wcp.tile([P, H], U32, tag="wc", name="wc%d" % e, align_bytes=64)
+            wss[e] = wcp.tile([P, H], U8, tag="ws", name="ws%d" % e, align_bytes=64)
+            nc.vector.quantize_mx(
+                out=wcs[e][:].bitcast(FP8X4), scales=wss[e][:], in_=wgs[e][:].rearrange("p h j -> p (h j)")
+            )
+            if e + 3 < E:
+                wload(e + 3)
+
+        gs = cst.tile([P, E, B, PACK], BF16, name="gs", align_bytes=64)
+        sc = cst.tile([P, E, B], U32, name="sc", align_bytes=64)
+        ss = cst.tile([P, E, B], U8, name="ss", align_bytes=64)
+        accs = {}
+
+        def share_op(t, i, n):
+            if n == 0:
+                accs[(t, i)] = acp.tile([P, D], F32, tag="acc%d" % i, name="acc%d_%d" % (t, i))
+                nc.vector.tensor_scalar_mul(out=accs[(t, i)][:], in0=tns[t][:, 0, :], scalar1=dn[:, t, i, 0:1])
+            else:
+                nc.vector.scalar_tensor_tensor(
+                    out=accs[(t, i)][:], in0=tns[t][:, n, :], scalar=dn[:, t, i, n:n + 1], in1=accs[(t, i)][:],
+                    op0=ALU.mult, op1=ALU.add,
+                )
+
+        def share_end(t, i):
+            e = EP + i
+            pst = psH.tile([P, PACK, P], F32, tag="ph", name="pst%d_%d" % (t, i))
+            for j in range(PACK):
+                nc.tensor.transpose(pst[:, j, :], accs[(t, i)][:, P * j:P * j + P], ident[:])
+            nc.vector.tensor_copy(out=gs[:, e, P * t:P * t + P, :], in_=pst[:].rearrange("p j b -> p b j"))
+
+        def share_quant(t, i):
+            e = EP + i
+            nc.vector.quantize_mx(
+                out=sc[:, e, P * t:P * t + P].bitcast(FP8X4),
+                scales=ss[:, e, P * t:P * t + P],
+                in_=gs[:, e, P * t:P * t + P, :].rearrange("p b j -> p (b j)"),
+            )
+
+        share0 = [(0, i, n) for n in range(NA) for i in range(NV)]
+
+        for g in range(G):
+            ps = psH.tile([P, PACK, EP * GB], F32, tag="ph", name="ps%d" % g)
+            for j in range(PACK):
+                nc.tensor.matmul(
+                    ps[:, j, :],
+                    lhsT=tfs[g // 4][:, g % 4, P * j:P * j + P],
+                    rhs=dblk[:, g, :, :].rearrange("p e b -> p (e b)"),
+                    start=True,
+                    stop=True,
+                )
+            nc.scalar.copy(
+                out=gs[:, 0:EP, GB * g:GB * g + GB, :],
+                in_=ps[:].rearrange("p j (e b) -> p e b j", e=EP),
+            )
+            if g in ACT_STEP:
+                e, c0 = ACT_STEP[g]
+                if c0 == HV[e]:
+                    regroup(nc.vector.tensor_copy, e, 0, HV[e])
+                regroup(nc.scalar.copy, e, c0, c0 + 256)
+                if c0 + 256 == H:
+                    wquant(e)
+            if g >= 4:
+                for item in share0[2 * (g - 4):2 * (g - 4) + 2]:
+                    share_op(item[0], item[1], item[2])
+        tnload(1)
+
+        def squant(m):
+            nc.vector.quantize_mx(
+                out=sc[:, 2 * m:2 * m + 2, :].rearrange("p e b -> p (e b)").bitcast(FP8X4),
+                scales=ss[:, 2 * m:2 * m + 2, :].rearrange("p e b -> p (e b)"),
+                in_=gs[:, 2 * m:2 * m + 2, :, :].rearrange("p e b j -> p (e b j)"),
+            )
+
+        squant(0)
+
+        fills = []
+        fills.append((1, 0.5, lambda: squant(1)))
+        for e in (4, 5):
+            fills.append((2, 0.9, lambda e=e: regroup(nc.vector.tensor_copy, e, 0, 512)))
+            fills.append((2, 0.9, lambda e=e: regroup(nc.vector.tensor_copy, e, 512, H)))
+            fills.append((2, 0.9, lambda e=e: wquant(e)))
+        fills.append((2, 0.5, lambda: squant(2)))
+        for i in range(NV):
+            fills.append((3, 0.5, lambda i=i: share_end(0, i)))
+        for n in range(NA):
+            for i in range(NV):
+                fills.append((3, 0.5, lambda i=i, n=n: share_op(1, i, n)))
+        for i in range(NV):
+            fills.append((3, 0.2, lambda i=i: share_quant(0, i)))
+        for i in range(NV):
+            fills.append((3, 0.5, lambda i=i: share_end(1, i)))
+        for e in (6, 7):
+            fills.append((3, 0.9, lambda e=e: regroup(nc.vector.tensor_copy, e, 0, 512)))
+            fills.append((3, 0.9, lambda e=e: regroup(nc.vector.tensor_copy, e, 512, H)))
+            fills.append((3, 0.9, lambda e=e: wquant(e)))
+        for i in range(NV):
+            fills.append((3, 0.2, lambda i=i: share_quant(1, i)))
+        pos = [0]
+
+        def fill(budget):
+            spent = 0.0
+            while pos[0] < len(fills) and spent < budget:
+                item = fills[pos[0]]
+                pos[0] = pos[0] + 1
+                item[2]()
+                spent += item[1]
+
+        def need(k):
+            last = -1
+            for idx in range(pos[0], len(fills)):
+                if fills[idx][0] <= k:
+                    last = idx
+            while pos[0] <= last:
+                item = fills[pos[0]]
+                pos[0] = pos[0] + 1
+                item[2]()
+
+        xs, us, negmus, vss, rstds = {}, {}, {}, {}, {}
+        junk = cst.tile([P, H], BF16, name="junk")
+        out_v = out.rearrange("(t b) e h -> b t e h", b=P)
+
+        def mxa(e, t):
+            if t == 0:
+                xs[e] = xp.tile([P, 2, H], F32, tag="x", name="x%d" % e)
+                negmus[e] = stp.tile([P, 2], F32, tag="negmu", name="negmu%d" % e)
+            s01 = stp.tile([P, 2], F32, tag="s01", name="s01_%d_%d" % (e, t))
+            for hh in range(2):
+                ph = psH.tile([P, 512], F32, tag="ph", name="ph%d_%d_%d" % (e, t, hh))
+                nc.tensor.matmul_mx(
+                    out=ph[:],
+                    lhsT=sc[:, e, P * t:P * t + P].bitcast(FP8X4),
+                    lhsT_scale=ss[:, e, P * t:P * t + P],
+                    rhs=wcs[e][:, 512 * hh:512 * hh + 512].bitcast(FP8X4),
+                    rhs_scale=wss[e][:, 512 * hh:512 * hh + 512],
+                    start=True,
+                    stop=True,
+                )
+                nc.vector.scalar_tensor_tensor(
+                    out=xs[e][:, t, 512 * hh:512 * hh + 512],
+                    in0=ph[:],
+                    scalar=1.0,
+                    in1=bbs[e][:, 512 * hh:512 * hh + 512],
+                    op0=ALU.mult,
+                    op1=ALU.add,
+                    accum_out=s01[:, hh:hh + 1],
+                )
+            nc.vector.tensor_scalar(
+                out=negmus[e][:, t:t + 1], in0=s01[:, 0:1], scalar1=s01[:, 1:2], scalar2=-1.0 / H,
+                op0=ALU.add, op1=ALU.mult,
+            )
+            if t == 1 and e + 3 < E:
+                bload(e + 3, nc.sync)
+
+        def cc(e, t):
+            if t == 0:
+                us[e] = up.tile([P, 2, H], F32, tag="u", name="u%d" % e)
+            nc.vector.scalar_tensor_tensor(
+                out=us[e][:, t, :], in0=xs[e][:, t, :], scalar=negmus[e][:, t:t + 1], in1=pgs[e][:],
+                op0=ALU.add, op1=ALU.mult,
+            )
+
+        def sq(e):
+            vss[e] = stp.tile([P, 2], F32, tag="vs", name="vs%d" % e)
+            for t in range(2):
+                nc.scalar.activation(
+                    out=junk[:], in_=xs[e][:, t, :], func=ACT.Square, bias=negmus[e][:, t:t + 1],
+                    accum_out=vss[e][:, t:t + 1],
+                )
+            ve = stp.tile([P, 2], F32, tag="ve", name="ve%d" % e)
+            rstds[e] = stp.tile([P, 2], F32, tag="rstd", name="rstd%d" % e)
+            nc.gpsimd.tensor_scalar(out=ve[:], in0=vss[e][:], scalar1=1.0 / H, scalar2=EPS, op0=ALU.mult, op1=ALU.add)
+            nc.gpsimd.tensor_tensor(out=rstds[e][:], in0=ve[:], in1=mhalf[:], op=ALU.pow)
+
+        def dd(e):
+            for t in range(2):
+                nc.vector.scalar_tensor_tensor(
+                    out=xs[e][:, t, :], in0=us[e][:, t, :], scalar=rstds[e][:, t:t + 1], in1=pbs[e][:],
+                    op0=ALU.mult, op1=ALU.add,
+                )
+            if e + 2 < E:
+                peb(e + 2)
+
+        def flat(tl):
+            return tl[:].rearrange("p t h -> p (t h)")
+
+        def ex(e):
+            nc.scalar.activation(out=flat(us[e]), in_=flat(xs[e]), func=ACT.Exp)
+
+        def ln(e):
+            nc.scalar.activation(out=flat(us[e]), in_=flat(us[e]), func=ACT.Ln, bias=1.0)
+
+        def fin(e):
+            eng = nc.gpsimd if e in F_ON_POOL else nc.vector
+            if e < E - 2:
+                nc.scalar.activation(out=flat(us[e]), in_=flat(us[e]), func=ACT.Tanh)
+                for t in range(2):
+                    eng.tensor_tensor(out=us[e][:, t, :], in0=xs[e][:, t, :], in1=us[e][:, t, :], op=ALU.mult)
+                nc.sync.dma_start(out=out_v[:, :, e, :], in_=us[e][:])
+            else:
+                for t in range(2):
+                    nc.scalar.activation(out=us[e][:, t, :], in_=us[e][:, t, :], func=ACT.Tanh)
+                    eng.tensor_tensor(out=us[e][:, t, :], in0=xs[e][:, t, :], in1=us[e][:, t, :], op=ALU.mult)
+                    nc.sync.dma_start(out=out_v[:, t, e, :], in_=us[e][:, t, :])
+
+        def head(k):
+            need(k)
+            for e in (2 * k, 2 * k + 1):
+                mxa(e, 0)
+                mxa(e, 1)
+                cc(e, 0)
+                cc(e, 1)
+
+        NBATCH = E // 2
+        head(0)
+        for k in range(-1, NBATCH):
+            nxt = k + 1 < NBATCH
+            if k >= 0:
+                ln(2 * k)
+            if nxt:
+                sq(2 * k + 2)
+            fill(FILL1)
+            if nxt:
+                dd(2 * k + 2)
+            if k >= 0:
+                ln(2 * k + 1)
+            if nxt:
+                sq(2 * k + 3)
+            fill(FILL2)
+            if nxt:
+                dd(2 * k + 3)
+            if k >= 0:
+                fin(2 * k)
+                fin(2 * k + 1)
+            if nxt:
+                ex(2 * k + 2)
+                ex(2 * k + 3)
+            if k + 2 < NBATCH:
+                head(k + 2)
+            fill(FILL3)

@@ -19,11 +19,20 @@ GB = 16
 PACK = 4
 EPS = 1e-5
 EP = 6
-HV = (512, 512, 256, 256, 1024, 1024, 1024, 1024)
-ACT_STEP = {0: (0, 512), 1: (0, 768), 2: (1, 512), 3: (1, 768), 6: (2, 256), 7: (2, 512), 8: (2, 768),
-            10: (3, 256), 11: (3, 512), 12: (3, 768)}
-F_ON_POOL = (0, 1, 2, 3, 4, 5)
-FILL1, FILL2, FILL3 = 2.0, 2.0, 2.5
+NV = E - EP
+CH = 256
+HV = (1024, 1024, 1024, 1024, 1024, 1024, 1024, 1024)
+BATCHES = ((0, 1), (2, 3), (4, 5), (6, 7))
+F_ON_POOL = (0, 1, 2, 3, 4)
+SPLIT_FIN = (6, 7)
+ACT_CASTS = (1, 2, 3)
+FRONT_CHUNKS = (0, 0, 0, 0, 0, 0, 0, 0, 0, 0, 0, 0, 0, 0, 0, 0)
+FRONT_SHARE = (0, 0, 0, 0, 0, 0, 0, 0, 0, 0, 0, 0, 0, 0, 0, 0)
+PRO_CHUNKS = (0, 0, 0)
+FILL1, FILL3 = 0.0, 5.0
+SHARE_END_ACT = False
+SHARE_POOL = (0, 1)
+STATS_DVE = ()
 
 FLOPS = 2 * E * B * D * H + 2 * B * NA * E * D
 
@@ -34,13 +43,14 @@ def tile_softmoedynamics_pa_kernel(tc, tokens, logits, W1, b1, g1, be1, out):
         cst = ctx.enter_context(tc.tile_pool(name="cst", bufs=1))
         xp = ctx.enter_context(tc.tile_pool(name="xp", bufs=6))
         up = ctx.enter_context(tc.tile_pool(name="up", bufs=6))
-        tnp = ctx.enter_context(tc.tile_pool(name="tnp", bufs=1))
+        tnp = ctx.enter_context(tc.tile_pool(name="tnp", bufs=2))
         wrp = ctx.enter_context(tc.tile_pool(name="wrp", bufs=3))
         wgp = ctx.enter_context(tc.tile_pool(name="wgp", bufs=2))
-        wcp = ctx.enter_context(tc.tile_pool(name="wcp", bufs=5))
+        wcp = ctx.enter_context(tc.tile_pool(name="wcp", bufs=4))
         bbp = ctx.enter_context(tc.tile_pool(name="bbp", bufs=3))
         acp = ctx.enter_context(tc.tile_pool(name="acp", bufs=1))
         stp = ctx.enter_context(tc.tile_pool(name="stp", bufs=8))
+        tmp_pool = ctx.enter_context(tc.tile_pool(name="tmp_pool", bufs=2))
         psH = ctx.enter_context(tc.psum_pool(name="psH", bufs=4))
         psG = ctx.enter_context(tc.psum_pool(name="psG", bufs=2))
         ctx.enter_context(tc.manual_schedule())
@@ -49,8 +59,8 @@ def tile_softmoedynamics_pa_kernel(tc, tokens, logits, W1, b1, g1, be1, out):
         make_identity(nc, ident[:])
         identb = cst.tile([P, P], BF16, name="identb")
         make_identity(nc, identb[:])
-        mhalf = cst.tile([P, 2], F32, name="mhalf")
-        nc.gpsimd.memset(mhalf[:], -0.5)
+        epst = cst.tile([P, 1], F32, name="epst")
+        nc.gpsimd.memset(epst[:], EPS)
 
         lg_raw = cst.tile([P, G, 16], BF16, name="lg_raw")
         nc.sync.dma_start(out=lg_raw[:, :, 0:E], in_=logits.rearrange("(g b) n e -> (b n) g e", b=GB))
@@ -83,12 +93,25 @@ def tile_softmoedynamics_pa_kernel(tc, tokens, logits, W1, b1, g1, be1, out):
             nc.sync.dma_start(out=tn[:], in_=tokens[P * t:P * t + P])
             tns[t] = tn
 
-        wload(0)
-        wload(1)
-        tnload(0)
-        wload(2)
+        for what in (0, 1, 10, 2, 11):
+            if what >= 10:
+                tnload(what - 10)
+            else:
+                wload(what)
         for e in range(3):
             bload(e, nc.gpsimd)
+
+        pgs, pbs = {}, {}
+
+        def peb(e):
+            pg = psG.tile([P, H], BF16, tag="pg", name="pg%d" % e)
+            pb = psG.tile([P, H], BF16, tag="pb", name="pb%d" % e)
+            for w, dst in ((0, pg), (1, pb)):
+                for c in range(8):
+                    col = 64 * w + 8 * e + c
+                    nc.tensor.transpose(dst[:, P * c:P * c + P], gcol[:, col:col + 1].to_broadcast([P, P]), identb[:])
+            pgs[e] = pg
+            pbs[e] = pb
 
         mask = cst.tile([P, GB], F32, name="mask")
         nc.vector.tensor_reduce(out=mask[:], in_=ident[:].rearrange("p (b n) -> p b n", n=NA), axis=AX.X, op=ALU.add)
@@ -103,15 +126,19 @@ def tile_softmoedynamics_pa_kernel(tc, tokens, logits, W1, b1, g1, be1, out):
         sh = cst.tile([P, GB, NA], F32, name="sh")
         nc.vector.tensor_tensor(out=sh[:], in0=psT[:], in1=mx[:].unsqueeze(2).to_broadcast([P, GB, NA]), op=ALU.subtract)
         nc.scalar.activation(out=sh[:], in_=sh[:], func=ACT.Exp)
+        gcol = cst.tile([P, P], BF16, name="gcol")
+        nc.vector.tensor_copy(out=gcol[:], in_=psR[:])
+        peb(0)
+        peb(1)
 
-        tfs = []
+        dn = cst.tile([P, 2, NV, NA], F32, name="dn")
+        dnv = dn[:].rearrange("b t e n -> b (t e) n")
+        nc.vector.tensor_copy(out=dn[:], in_=lgn[:].rearrange("b t (n e) -> b t e n", e=E)[:, :, EP:E, :])
+        mxn = cst.tile([P, 2 * NV], F32, name="mxn")
+        nc.vector.tensor_reduce(out=mxn[:], in_=dnv, axis=AX.X, op=ALU.max)
+        nc.vector.tensor_tensor(out=dnv, in0=dnv, in1=mxn[:].unsqueeze(2).to_broadcast([P, 2 * NV, NA]), op=ALU.subtract)
+        nc.scalar.activation(out=dnv, in_=dnv, func=ACT.Exp)
 
-        def cast(q):
-            tf = xp.tile([P, 4, D], F32, tag="x", name="tf%d" % q)
-            nc.vector.tensor_copy(out=tf[:], in_=trs[q][:])
-            tfs.append(tf)
-
-        cast(0)
         sm = cst.tile([P, GB], F32, name="sm")
         nc.vector.tensor_reduce(out=sm[:], in_=sh[:], axis=AX.X, op=ALU.add)
         rs = cst.tile([P, GB], F32, name="rs")
@@ -119,9 +146,22 @@ def tile_softmoedynamics_pa_kernel(tc, tokens, logits, W1, b1, g1, be1, out):
         nc.vector.tensor_tensor(out=sh[:], in0=sh[:], in1=rs[:].unsqueeze(2).to_broadcast([P, GB, NA]), op=ALU.mult)
         psD = psH.tile([P, G, E], F32, tag="ph", name="psD")
         nc.tensor.transpose(psD[:].rearrange("p g e -> p (g e)"), sh[:].rearrange("p b n -> p (b n)"), ident[:])
-        gcol = cst.tile([P, P], BF16, name="gcol")
-        nc.vector.tensor_copy(out=gcol[:], in_=psR[:])
-        cast(1)
+        smn = cst.tile([P, 2 * NV], F32, name="smn")
+        nc.vector.tensor_reduce(out=smn[:], in_=dnv, axis=AX.X, op=ALU.add)
+        rsn = cst.tile([P, 2 * NV], F32, name="rsn")
+        nc.vector.reciprocal(out=rsn[:], in_=smn[:])
+        nc.vector.tensor_tensor(out=dnv, in0=dnv, in1=rsn[:].unsqueeze(2).to_broadcast([P, 2 * NV, NA]), op=ALU.mult)
+
+        tfs = []
+
+        def cast(q):
+            tf = xp.tile([P, 4, D], F32, tag="x", name="tf%d" % q)
+            if q in ACT_CASTS:
+                nc.scalar.copy(out=tf[:], in_=trs[q][:])
+            else:
+                nc.vector.tensor_copy(out=tf[:], in_=trs[q][:])
+            tfs.append(tf)
+
         dblk = cst.tile([P, G, EP, GB], F32, name="dblk")
         for g0 in (0, 8):
             nc.vector.tensor_tensor(
@@ -130,37 +170,10 @@ def tile_softmoedynamics_pa_kernel(tc, tokens, logits, W1, b1, g1, be1, out):
                 in1=mask[:].unsqueeze(1).unsqueeze(1).to_broadcast([P, 8, EP, GB]),
                 op=ALU.mult,
             )
-        cast(2)
-        cast(3)
-
-        NV = E - EP
-        dn = cst.tile([P, 2, NV, NA], F32, name="dn")
-        dnv = dn[:].rearrange("b t e n -> b (t e) n")
-        nc.vector.tensor_copy(out=dn[:], in_=lgn[:].rearrange("b t (n e) -> b t e n", e=E)[:, :, EP:E, :])
-        mxn = cst.tile([P, 2 * NV], F32, name="mxn")
-        nc.vector.tensor_reduce(out=mxn[:], in_=dnv, axis=AX.X, op=ALU.max)
-        nc.vector.tensor_tensor(out=dnv, in0=dnv, in1=mxn[:].unsqueeze(2).to_broadcast([P, 2 * NV, NA]), op=ALU.subtract)
-        nc.scalar.activation(out=dnv, in_=dnv, func=ACT.Exp)
-        smn = cst.tile([P, 2 * NV], F32, name="smn")
-        nc.vector.tensor_reduce(out=smn[:], in_=dnv, axis=AX.X, op=ALU.add)
-        rsn = cst.tile([P, 2 * NV], F32, name="rsn")
-        nc.vector.reciprocal(out=rsn[:], in_=smn[:])
-        nc.vector.tensor_tensor(out=dnv, in0=dnv, in1=rsn[:].unsqueeze(2).to_broadcast([P, 2 * NV, NA]), op=ALU.mult)
-
-        pgs, pbs = {}, {}
-
-        def peb(e):
-            pg = psG.tile([P, H], BF16, tag="pg", name="pg%d" % e)
-            pb = psG.tile([P, H], BF16, tag="pb", name="pb%d" % e)
-            for w, dst in ((0, pg), (1, pb)):
-                for c in range(8):
-                    col = 64 * w + 8 * e + c
-                    nc.tensor.transpose(dst[:, P * c:P * c + P], gcol[:, col:col + 1].to_broadcast([P, P]), identb[:])
-            pgs[e] = pg
-            pbs[e] = pb
-
-        peb(0)
-        peb(1)
+            if g0 == 0:
+                cast(0)
+        for q in range(1, 4):
+            cast(q)
 
         def regroup(copy_fn, e, c0, c1):
             if e not in wgs:
@@ -170,7 +183,19 @@ def tile_softmoedynamics_pa_kernel(tc, tokens, logits, W1, b1, g1, be1, out):
                 in_=wrs[e][:, :, c0:c1].rearrange("p t (c i) -> p c t i", i=4),
             )
 
+        achunks = [(e, c0) for e in range(E) for c0 in range(HV[e], H, CH)]
+        apos = [0]
+
+        def afill(n):
+            while n > 0 and apos[0] < len(achunks):
+                e, c0 = achunks[apos[0]]
+                apos[0] = apos[0] + 1
+                regroup(nc.scalar.copy, e, c0, c0 + CH)
+                n -= 1
+
         def wquant(e):
+            while apos[0] < len(achunks) and achunks[apos[0]][0] <= e:
+                afill(1)
             wcs[e] = wcp.tile([P, H], U32, tag="wc", name="wc%d" % e, align_bytes=64)
             wss[e] = wcp.tile([P, H], U8, tag="ws", name="ws%d" % e, align_bytes=64)
             nc.vector.quantize_mx(
@@ -186,7 +211,17 @@ def tile_softmoedynamics_pa_kernel(tc, tokens, logits, W1, b1, g1, be1, out):
 
         def share_op(t, i, n):
             if n == 0:
-                accs[(t, i)] = acp.tile([P, D], F32, tag="acc%d" % i, name="acc%d_%d" % (t, i))
+                accs[(t, i)] = acp.tile([P, D], F32, tag="acc%d_%d" % (t, i), name="acc%d_%d" % (t, i))
+            if i in SHARE_POOL:
+                dst = accs[(t, i)]
+                if n > 0:
+                    dst = tmp_pool.tile([P, D], F32, tag="tmp", name="tmp%d_%d_%d" % (t, i, n))
+                nc.gpsimd.tensor_scalar(
+                    out=dst[:], in0=tns[t][:, n, :], scalar1=dn[:, t, i, n:n + 1], scalar2=0.0, op0=ALU.mult, op1=ALU.add
+                )
+                if n > 0:
+                    nc.gpsimd.tensor_tensor(out=accs[(t, i)][:], in0=accs[(t, i)][:], in1=dst[:], op=ALU.add)
+            elif n == 0:
                 nc.vector.tensor_scalar_mul(out=accs[(t, i)][:], in0=tns[t][:, 0, :], scalar1=dn[:, t, i, 0:1])
             else:
                 nc.vector.scalar_tensor_tensor(
@@ -199,17 +234,71 @@ def tile_softmoedynamics_pa_kernel(tc, tokens, logits, W1, b1, g1, be1, out):
             pst = psH.tile([P, PACK, P], F32, tag="ph", name="pst%d_%d" % (t, i))
             for j in range(PACK):
                 nc.tensor.transpose(pst[:, j, :], accs[(t, i)][:, P * j:P * j + P], ident[:])
-            nc.vector.tensor_copy(out=gs[:, e, P * t:P * t + P, :], in_=pst[:].rearrange("p j b -> p b j"))
+            copy_fn = nc.scalar.copy if SHARE_END_ACT else nc.vector.tensor_copy
+            copy_fn(out=gs[:, e, P * t:P * t + P, :], in_=pst[:].rearrange("p j b -> p b j"))
 
-        def share_quant(t, i):
+        def share_quant(i):
             e = EP + i
             nc.vector.quantize_mx(
-                out=sc[:, e, P * t:P * t + P].bitcast(FP8X4),
-                scales=ss[:, e, P * t:P * t + P],
-                in_=gs[:, e, P * t:P * t + P, :].rearrange("p b j -> p (b j)"),
+                out=sc[:, e, :].bitcast(FP8X4), scales=ss[:, e, :], in_=gs[:, e, :, :].rearrange("p b j -> p (b j)")
             )
 
-        share0 = [(0, i, n) for n in range(NA) for i in range(NV)]
+        def squant(m):
+            nc.vector.quantize_mx(
+                out=sc[:, 2 * m:2 * m + 2, :].rearrange("p e b -> p (e b)").bitcast(FP8X4),
+                scales=ss[:, 2 * m:2 * m + 2, :].rearrange("p e b -> p (e b)"),
+                in_=gs[:, 2 * m:2 * m + 2, :, :].rearrange("p e b j -> p (e b j)"),
+            )
+
+        fills = []
+        for t in range(2):
+            for n in range(NA):
+                for i in range(NV):
+                    if i not in SHARE_POOL:
+                        fills.append((EP, 0.5, lambda t=t, i=i, n=n: share_op(t, i, n)))
+        nshare = len(fills)
+        order = (0, 1, 2, 3, "s1", 4, 5, "s2", 6, 7, "se", "sq")
+        for e in order:
+            if e == "s1":
+                fills.append((2, 0.5, lambda: squant(1), "s"))
+            elif e == "s2":
+                fills.append((4, 0.5, lambda: squant(2), "s"))
+            elif e == "se":
+                for t in range(2):
+                    for i in range(NV):
+                        fills.append((EP, 0.5, lambda t=t, i=i: share_end(t, i)))
+            elif e == "sq":
+                for i in range(NV):
+                    fills.append((EP + i, 0.25, lambda i=i: share_quant(i)))
+            else:
+                for c0 in range(0, HV[e], 512):
+                    fills.append((e, 0.9, lambda e=e, c0=c0: regroup(nc.vector.tensor_copy, e, c0, min(c0 + 512, HV[e])), "w"))
+                fills.append((e, 0.9, lambda e=e: wquant(e), "w"))
+        pos = [0]
+        done = set()
+
+        def run(idx):
+            if idx not in done:
+                done.add(idx)
+                fills[idx][2]()
+
+        def fill(budget):
+            spent = 0.0
+            while pos[0] < len(fills) and spent < budget:
+                if pos[0] not in done:
+                    spent += fills[pos[0]][1]
+                run(pos[0])
+                pos[0] = pos[0] + 1
+
+        def need(e, kind=None):
+            for idx in range(len(fills)):
+                if fills[idx][0] <= e and (kind is None or fills[idx][-1] == kind):
+                    run(idx)
+
+        for t in range(2):
+            for i in SHARE_POOL:
+                for n in range(NA):
+                    share_op(t, i, n)
 
         for g in range(G):
             ps = psH.tile([P, PACK, EP * GB], F32, tag="ph", name="ps%d" % g)
@@ -225,70 +314,14 @@ def tile_softmoedynamics_pa_kernel(tc, tokens, logits, W1, b1, g1, be1, out):
                 out=gs[:, 0:EP, GB * g:GB * g + GB, :],
                 in_=ps[:].rearrange("p j (e b) -> p e b j", e=EP),
             )
-            if g in ACT_STEP:
-                e, c0 = ACT_STEP[g]
-                if c0 == HV[e]:
-                    regroup(nc.vector.tensor_copy, e, 0, HV[e])
-                regroup(nc.scalar.copy, e, c0, c0 + 256)
-                if c0 + 256 == H:
-                    wquant(e)
-            if g >= 4:
-                for item in share0[2 * (g - 4):2 * (g - 4) + 2]:
-                    share_op(item[0], item[1], item[2])
-        tnload(1)
-
-        def squant(m):
-            nc.vector.quantize_mx(
-                out=sc[:, 2 * m:2 * m + 2, :].rearrange("p e b -> p (e b)").bitcast(FP8X4),
-                scales=ss[:, 2 * m:2 * m + 2, :].rearrange("p e b -> p (e b)"),
-                in_=gs[:, 2 * m:2 * m + 2, :, :].rearrange("p e b j -> p (e b j)"),
-            )
-
+            afill(FRONT_CHUNKS[g])
+            for w in range(FRONT_SHARE[g]):
+                fill(0.1)
+            if g in {1: 0, 4: 1, 9: 2}:
+                need({1: 0, 4: 1, 9: 2}[g], "w")
         squant(0)
 
-        fills = []
-        fills.append((1, 0.5, lambda: squant(1)))
-        for e in (4, 5):
-            fills.append((2, 0.9, lambda e=e: regroup(nc.vector.tensor_copy, e, 0, 512)))
-            fills.append((2, 0.9, lambda e=e: regroup(nc.vector.tensor_copy, e, 512, H)))
-            fills.append((2, 0.9, lambda e=e: wquant(e)))
-        fills.append((2, 0.5, lambda: squant(2)))
-        for i in range(NV):
-            fills.append((3, 0.5, lambda i=i: share_end(0, i)))
-        for n in range(NA):
-            for i in range(NV):
-                fills.append((3, 0.5, lambda i=i, n=n: share_op(1, i, n)))
-        for i in range(NV):
-            fills.append((3, 0.2, lambda i=i: share_quant(0, i)))
-        for i in range(NV):
-            fills.append((3, 0.5, lambda i=i: share_end(1, i)))
-        for e in (6, 7):
-            fills.append((3, 0.9, lambda e=e: regroup(nc.vector.tensor_copy, e, 0, 512)))
-            fills.append((3, 0.9, lambda e=e: regroup(nc.vector.tensor_copy, e, 512, H)))
-            fills.append((3, 0.9, lambda e=e: wquant(e)))
-        for i in range(NV):
-            fills.append((3, 0.2, lambda i=i: share_quant(1, i)))
-        pos = [0]
-
-        def fill(budget):
-            spent = 0.0
-            while pos[0] < len(fills) and spent < budget:
-                item = fills[pos[0]]
-                pos[0] = pos[0] + 1
-                item[2]()
-                spent += item[1]
-
-        def need(k):
-            last = -1
-            for idx in range(pos[0], len(fills)):
-                if fills[idx][0] <= k:
-                    last = idx
-            while pos[0] <= last:
-                item = fills[pos[0]]
-                pos[0] = pos[0] + 1
-                item[2]()
-
-        xs, us, negmus, vss, rstds = {}, {}, {}, {}, {}
+        xs, us, negmus, vss, rstds, mvs = {}, {}, {}, {}, {}, {}
         junk = cst.tile([P, H], BF16, name="junk")
         out_v = out.rearrange("(t b) e h -> b t e h", b=P)
 
@@ -315,39 +348,68 @@ def tile_softmoedynamics_pa_kernel(tc, tokens, logits, W1, b1, g1, be1, out):
                     in1=bbs[e][:, 512 * hh:512 * hh + 512],
                     op0=ALU.mult,
                     op1=ALU.add,
-                    accum_out=s01[:, hh:hh + 1],
+                    accum_out=None if e in STATS_DVE else s01[:, hh:hh + 1],
                 )
-            nc.vector.tensor_scalar(
-                out=negmus[e][:, t:t + 1], in0=s01[:, 0:1], scalar1=s01[:, 1:2], scalar2=-1.0 / H,
-                op0=ALU.add, op1=ALU.mult,
-            )
+            if e not in STATS_DVE:
+                nc.vector.tensor_scalar(
+                    out=negmus[e][:, t:t + 1], in0=s01[:, 0:1], scalar1=s01[:, 1:2], scalar2=-1.0 / H,
+                    op0=ALU.add, op1=ALU.mult,
+                )
             if t == 1 and e + 3 < E:
                 bload(e + 3, nc.sync)
+
+        def bn(e, t):
+            if t == 0:
+                mvs[e] = stp.tile([P, 2, 2], F32, tag="mv", name="mv%d" % e)
+            st6 = stp.tile([P, 2, 6], F32, tag="st6", name="st6_%d_%d" % (e, t))
+            for hh in range(2):
+                nc.vector.bn_stats(out=st6[:, hh, :], in_=xs[e][:, t, 512 * hh:512 * hh + 512])
+            nc.vector.bn_aggr(out=mvs[e][:, t, :], in_=st6[:].rearrange("p a s -> p (a s)"))
 
         def cc(e, t):
             if t == 0:
                 us[e] = up.tile([P, 2, H], F32, tag="u", name="u%d" % e)
-            nc.vector.scalar_tensor_tensor(
-                out=us[e][:, t, :], in0=xs[e][:, t, :], scalar=negmus[e][:, t:t + 1], in1=pgs[e][:],
-                op0=ALU.add, op1=ALU.mult,
-            )
+            if e in STATS_DVE:
+                nc.vector.scalar_tensor_tensor(
+                    out=us[e][:, t, :], in0=xs[e][:, t, :], scalar=mvs[e][:, t, 0:1], in1=pgs[e][:],
+                    op0=ALU.subtract, op1=ALU.mult,
+                )
+            else:
+                nc.vector.scalar_tensor_tensor(
+                    out=us[e][:, t, :], in0=xs[e][:, t, :], scalar=negmus[e][:, t:t + 1], in1=pgs[e][:],
+                    op0=ALU.add, op1=ALU.mult,
+                )
 
-        def sq(e):
-            vss[e] = stp.tile([P, 2], F32, tag="vs", name="vs%d" % e)
+        def sq(k, i):
+            e = BATCHES[k][i]
+            if i == 0:
+                vss[k] = stp.tile([P, 2 * len(BATCHES[k])], F32, tag="vs", name="vs%d" % k)
             for t in range(2):
+                if e in STATS_DVE:
+                    continue
                 nc.scalar.activation(
                     out=junk[:], in_=xs[e][:, t, :], func=ACT.Square, bias=negmus[e][:, t:t + 1],
-                    accum_out=vss[e][:, t:t + 1],
+                    accum_out=vss[k][:, 2 * i + t:2 * i + t + 1],
                 )
-            ve = stp.tile([P, 2], F32, tag="ve", name="ve%d" % e)
-            rstds[e] = stp.tile([P, 2], F32, tag="rstd", name="rstd%d" % e)
-            nc.gpsimd.tensor_scalar(out=ve[:], in0=vss[e][:], scalar1=1.0 / H, scalar2=EPS, op0=ALU.mult, op1=ALU.add)
-            nc.gpsimd.tensor_tensor(out=rstds[e][:], in0=ve[:], in1=mhalf[:], op=ALU.pow)
 
-        def dd(e):
+        def rstd_of(k):
+            lv = stp.tile([P, 2 * len(BATCHES[k])], F32, tag="lv", name="lv%d" % k)
+            rstds[k] = stp.tile([P, 2 * len(BATCHES[k])], F32, tag="rstd", name="rstd%d" % k)
+            for i in range(len(BATCHES[k])):
+                e = BATCHES[k][i]
+                if e in STATS_DVE:
+                    nc.scalar.activation(out=lv[:, 2 * i:2 * i + 2], in_=mvs[e][:, :, 1], func=ACT.Ln, bias=epst[:])
+                else:
+                    nc.scalar.activation(
+                        out=lv[:, 2 * i:2 * i + 2], in_=vss[k][:, 2 * i:2 * i + 2], func=ACT.Ln, scale=1.0 / H, bias=epst[:]
+                    )
+            nc.scalar.activation(out=rstds[k][:], in_=lv[:], func=ACT.Exp, scale=-0.5)
+
+        def dd(k, i):
+            e = BATCHES[k][i]
             for t in range(2):
                 nc.vector.scalar_tensor_tensor(
-                    out=xs[e][:, t, :], in0=us[e][:, t, :], scalar=rstds[e][:, t:t + 1], in1=pbs[e][:],
+                    out=xs[e][:, t, :], in0=us[e][:, t, :], scalar=rstds[k][:, 2 * i + t:2 * i + t + 1], in1=pbs[e][:],
                     op0=ALU.mult, op1=ALU.add,
                 )
             if e + 2 < E:
@@ -364,7 +426,7 @@ def tile_softmoedynamics_pa_kernel(tc, tokens, logits, W1, b1, g1, be1, out):
 
         def fin(e):
             eng = nc.gpsimd if e in F_ON_POOL else nc.vector
-            if e < E - 2:
+            if e not in SPLIT_FIN:
                 nc.scalar.activation(out=flat(us[e]), in_=flat(us[e]), func=ACT.Tanh)
                 for t in range(2):
                     eng.tensor_tensor(out=us[e][:, t, :], in0=xs[e][:, t, :], in1=us[e][:, t, :], op=ALU.mult)
@@ -376,37 +438,39 @@ def tile_softmoedynamics_pa_kernel(tc, tokens, logits, W1, b1, g1, be1, out):
                     nc.sync.dma_start(out=out_v[:, t, e, :], in_=us[e][:, t, :])
 
         def head(k):
-            need(k)
-            for e in (2 * k, 2 * k + 1):
+            need(max(BATCHES[k]))
+            for e in BATCHES[k]:
                 mxa(e, 0)
                 mxa(e, 1)
+                if e in STATS_DVE:
+                    bn(e, 0)
+                    bn(e, 1)
                 cc(e, 0)
                 cc(e, 1)
 
-        NBATCH = E // 2
+        NB = len(BATCHES)
         head(0)
-        for k in range(-1, NBATCH):
-            nxt = k + 1 < NBATCH
-            if k >= 0:
-                ln(2 * k)
+        for c in range(-1, NB):
+            prev = BATCHES[c] if c >= 0 else ()
+            nxt = BATCHES[c + 1] if c + 1 < NB else ()
+            for i in range(max(len(prev), len(nxt))):
+                if i < len(prev):
+                    ln(prev[i])
+                if i < len(nxt):
+                    sq(c + 1, i)
+                    if c < 0:
+                        afill(PRO_CHUNKS[i])
             if nxt:
-                sq(2 * k + 2)
+                rstd_of(c + 1)
             fill(FILL1)
-            if nxt:
-                dd(2 * k + 2)
-            if k >= 0:
-                ln(2 * k + 1)
-            if nxt:
-                sq(2 * k + 3)
-            fill(FILL2)
-            if nxt:
-                dd(2 * k + 3)
-            if k >= 0:
-                fin(2 * k)
-                fin(2 * k + 1)
-            if nxt:
-                ex(2 * k + 2)
-                ex(2 * k + 3)
-            if k + 2 < NBATCH:
-                head(k + 2)
+            for i in range(len(nxt)):
+                dd(c + 1, i)
+            for e in prev:
+                fin(e)
+            for e in nxt:
+                ex(e)
+            if c < 0:
+                afill(PRO_CHUNKS[2])
+            if c + 2 < NB:
+                head(c + 2)
             fill(FILL3)

@@ -21,17 +21,19 @@ EPS = 1e-5
 EP = 6
 NV = E - EP
 CH = 256
-HV = (1024, 1024, 1024, 1024, 1024, 1024, 1024, 1024)
+HV = (1024, 1024, 512, 512, 512, 512, 512, 512)
 BATCHES = ((0, 1), (2, 3), (4, 5), (6, 7))
 F_ON_POOL = (0, 1, 2, 3, 4)
 SPLIT_FIN = (6, 7)
-ACT_CASTS = (1, 2, 3)
-FRONT_CHUNKS = (0, 0, 0, 0, 0, 0, 0, 0, 0, 0, 0, 0, 0, 0, 0, 0)
+ACT_CASTS = (1, 2)
+FRONT_CHUNKS = (0, 0, 0, 0, 1, 1, 1, 1, 1, 1, 1, 1, 0, 0, 0, 0)
 FRONT_SHARE = (0, 0, 0, 0, 0, 0, 0, 0, 0, 0, 0, 0, 0, 0, 0, 0)
-PRO_CHUNKS = (0, 0, 0)
-FILL1, FILL3 = 0.0, 5.0
+PRO_CHUNKS = (2, 2, 0)
+FILL1, FILL3 = 0, 5
 SHARE_END_ACT = False
-SHARE_POOL = (0, 1)
+NBIG = 10
+SQ_LATE = False
+RSTD_POOL = True
 STATS_DVE = ()
 
 FLOPS = 2 * E * B * D * H + 2 * B * NA * E * D
@@ -41,17 +43,16 @@ def tile_softmoedynamics_pa_kernel(tc, tokens, logits, W1, b1, g1, be1, out):
     nc = tc.nc
     with ExitStack() as ctx:
         cst = ctx.enter_context(tc.tile_pool(name="cst", bufs=1))
-        xp = ctx.enter_context(tc.tile_pool(name="xp", bufs=6))
-        up = ctx.enter_context(tc.tile_pool(name="up", bufs=6))
+        big = ctx.enter_context(tc.tile_pool(name="big", bufs=NBIG))
+        trp = ctx.enter_context(tc.tile_pool(name="trp", bufs=4))
+        wgp = ctx.enter_context(tc.tile_pool(name="wgp", bufs=3))
         tnp = ctx.enter_context(tc.tile_pool(name="tnp", bufs=2))
-        wrp = ctx.enter_context(tc.tile_pool(name="wrp", bufs=3))
-        wgp = ctx.enter_context(tc.tile_pool(name="wgp", bufs=2))
-        wcp = ctx.enter_context(tc.tile_pool(name="wcp", bufs=4))
+        wcp = ctx.enter_context(tc.tile_pool(name="wcp", bufs=E))
         bbp = ctx.enter_context(tc.tile_pool(name="bbp", bufs=3))
-        acp = ctx.enter_context(tc.tile_pool(name="acp", bufs=1))
+        prp = ctx.enter_context(tc.tile_pool(name="prp", bufs=4))
         stp = ctx.enter_context(tc.tile_pool(name="stp", bufs=8))
-        tmp_pool = ctx.enter_context(tc.tile_pool(name="tmp_pool", bufs=2))
-        psH = ctx.enter_context(tc.psum_pool(name="psH", bufs=4))
+        psH = ctx.enter_context(tc.psum_pool(name="psH", bufs=3))
+        psS = ctx.enter_context(tc.psum_pool(name="psS", bufs=1))
         psG = ctx.enter_context(tc.psum_pool(name="psG", bufs=2))
         ctx.enter_context(tc.manual_schedule())
 
@@ -59,8 +60,14 @@ def tile_softmoedynamics_pa_kernel(tc, tokens, logits, W1, b1, g1, be1, out):
         make_identity(nc, ident[:])
         identb = cst.tile([P, P], BF16, name="identb")
         make_identity(nc, identb[:])
+        mhalf = cst.tile([P, 8], F32, name="mhalf")
+        nc.gpsimd.memset(mhalf[:], -0.5)
         epst = cst.tile([P, 1], F32, name="epst")
         nc.gpsimd.memset(epst[:], EPS)
+
+        warm = cst.tile([P, 1], F32, name="warm")
+        nc.vector.memset(warm[:], 0.0)
+        nc.scalar.activation(out=warm[:], in_=warm[:], func=ACT.Exp)
 
         lg_raw = cst.tile([P, G, 16], BF16, name="lg_raw")
         nc.sync.dma_start(out=lg_raw[:, :, 0:E], in_=logits.rearrange("(g b) n e -> (b n) g e", b=GB))
@@ -72,14 +79,18 @@ def tile_softmoedynamics_pa_kernel(tc, tokens, logits, W1, b1, g1, be1, out):
         tok_view = tokens.rearrange("(g b) n d -> (b n) g d", b=GB)
         trs = []
         for q in range(4):
-            tr = up.tile([P, 4, D], BF16, tag="u", name="tr%d" % q)
+            tr = trp.tile([P, 4, D], BF16, tag="tr", name="tr%d" % q)
             nc.sync.dma_start(out=tr[:], in_=tok_view[:, 4 * q:4 * q + 4, :])
             trs.append(tr)
 
+        tfs = []
+        for q in range(4):
+            tf = big.tile([P, 4, D], F32, tag="big", name="tf%d" % q, align_bytes=64)
+            tfs.append(tf)
         wrs, wgs, wcs, wss, bbs, tns = {}, {}, {}, {}, {}, {}
 
         def wload(e):
-            wr = wrp.tile([P, PACK, H], BF16, tag="wr", name="wr%d" % e)
+            wr = big.tile([P, PACK, H], BF16, tag="big", name="wr%d" % e, align_bytes=64)
             nc.sync.dma_start(out=wr[:], in_=W1[e].rearrange("(j p) h -> p j h", p=P))
             wrs[e] = wr
 
@@ -93,7 +104,7 @@ def tile_softmoedynamics_pa_kernel(tc, tokens, logits, W1, b1, g1, be1, out):
             nc.sync.dma_start(out=tn[:], in_=tokens[P * t:P * t + P])
             tns[t] = tn
 
-        for what in (0, 1, 10, 2, 11):
+        for what in (0, 1, 2, 3, 4, 5):
             if what >= 10:
                 tnload(what - 10)
             else:
@@ -152,15 +163,11 @@ def tile_softmoedynamics_pa_kernel(tc, tokens, logits, W1, b1, g1, be1, out):
         nc.vector.reciprocal(out=rsn[:], in_=smn[:])
         nc.vector.tensor_tensor(out=dnv, in0=dnv, in1=rsn[:].unsqueeze(2).to_broadcast([P, 2 * NV, NA]), op=ALU.mult)
 
-        tfs = []
-
         def cast(q):
-            tf = xp.tile([P, 4, D], F32, tag="x", name="tf%d" % q)
             if q in ACT_CASTS:
-                nc.scalar.copy(out=tf[:], in_=trs[q][:])
+                nc.scalar.copy(out=tfs[q][:], in_=trs[q][:])
             else:
-                nc.vector.tensor_copy(out=tf[:], in_=trs[q][:])
-            tfs.append(tf)
+                nc.vector.tensor_copy(out=tfs[q][:], in_=trs[q][:])
 
         dblk = cst.tile([P, G, EP, GB], F32, name="dblk")
         for g0 in (0, 8):
@@ -174,6 +181,11 @@ def tile_softmoedynamics_pa_kernel(tc, tokens, logits, W1, b1, g1, be1, out):
                 cast(0)
         for q in range(1, 4):
             cast(q)
+        for what in (6, 7, 10, 11):
+            if what >= 10:
+                tnload(what - 10)
+            else:
+                wload(what)
 
         def regroup(copy_fn, e, c0, c1):
             if e not in wgs:
@@ -201,8 +213,6 @@ def tile_softmoedynamics_pa_kernel(tc, tokens, logits, W1, b1, g1, be1, out):
             nc.vector.quantize_mx(
                 out=wcs[e][:].bitcast(FP8X4), scales=wss[e][:], in_=wgs[e][:].rearrange("p h j -> p (h j)")
             )
-            if e + 3 < E:
-                wload(e + 3)
 
         gs = cst.tile([P, E, B, PACK], BF16, name="gs", align_bytes=64)
         sc = cst.tile([P, E, B], U32, name="sc", align_bytes=64)
@@ -210,32 +220,22 @@ def tile_softmoedynamics_pa_kernel(tc, tokens, logits, W1, b1, g1, be1, out):
         accs = {}
 
         def share_op(t, i, n):
+            pr = prp.tile([P, D], F32, tag="pr", name="pr%d_%d_%d" % (t, i, n))
+            nc.vector.tensor_scalar_mul(out=pr[:], in0=tns[t][:, n, :], scalar1=dn[:, t, i, n:n + 1])
             if n == 0:
-                accs[(t, i)] = acp.tile([P, D], F32, tag="acc%d_%d" % (t, i), name="acc%d_%d" % (t, i))
-            if i in SHARE_POOL:
-                dst = accs[(t, i)]
-                if n > 0:
-                    dst = tmp_pool.tile([P, D], F32, tag="tmp", name="tmp%d_%d_%d" % (t, i, n))
-                nc.gpsimd.tensor_scalar(
-                    out=dst[:], in0=tns[t][:, n, :], scalar1=dn[:, t, i, n:n + 1], scalar2=0.0, op0=ALU.mult, op1=ALU.add
-                )
-                if n > 0:
-                    nc.gpsimd.tensor_tensor(out=accs[(t, i)][:], in0=accs[(t, i)][:], in1=dst[:], op=ALU.add)
-            elif n == 0:
-                nc.vector.tensor_scalar_mul(out=accs[(t, i)][:], in0=tns[t][:, 0, :], scalar1=dn[:, t, i, 0:1])
-            else:
-                nc.vector.scalar_tensor_tensor(
-                    out=accs[(t, i)][:], in0=tns[t][:, n, :], scalar=dn[:, t, i, n:n + 1], in1=accs[(t, i)][:],
-                    op0=ALU.mult, op1=ALU.add,
-                )
-
-        def share_end(t, i):
-            e = EP + i
-            pst = psH.tile([P, PACK, P], F32, tag="ph", name="pst%d_%d" % (t, i))
+                accs[(t, i)] = psS.tile([P, PACK, P], F32, tag="pss", name="pss%d_%d" % (t, i))
             for j in range(PACK):
-                nc.tensor.transpose(pst[:, j, :], accs[(t, i)][:, P * j:P * j + P], ident[:])
-            copy_fn = nc.scalar.copy if SHARE_END_ACT else nc.vector.tensor_copy
-            copy_fn(out=gs[:, e, P * t:P * t + P, :], in_=pst[:].rearrange("p j b -> p b j"))
+                nc.tensor.matmul(
+                    accs[(t, i)][:, j, :],
+                    lhsT=pr[:, P * j:P * j + P],
+                    rhs=ident[:],
+                    is_transpose=True,
+                    start=(n == 0 and j == 0),
+                    stop=(n == NA - 1 and j == PACK - 1),
+                )
+            if n == NA - 1:
+                copy_fn = nc.scalar.copy if SHARE_END_ACT else nc.vector.tensor_copy
+                copy_fn(out=gs[:, EP + i, P * t:P * t + P, :], in_=accs[(t, i)][:].rearrange("p j b -> p b j"))
 
         def share_quant(i):
             e = EP + i
@@ -251,22 +251,17 @@ def tile_softmoedynamics_pa_kernel(tc, tokens, logits, W1, b1, g1, be1, out):
             )
 
         fills = []
-        for t in range(2):
-            for n in range(NA):
-                for i in range(NV):
-                    if i not in SHARE_POOL:
-                        fills.append((EP, 0.5, lambda t=t, i=i, n=n: share_op(t, i, n)))
-        nshare = len(fills)
-        order = (0, 1, 2, 3, "s1", 4, 5, "s2", 6, 7, "se", "sq")
+        order = (0, 1, 2, 3, 4, 5, "s1", 6, 7, "s2", "sh", "sq")
         for e in order:
             if e == "s1":
                 fills.append((2, 0.5, lambda: squant(1), "s"))
             elif e == "s2":
                 fills.append((4, 0.5, lambda: squant(2), "s"))
-            elif e == "se":
+            elif e == "sh":
                 for t in range(2):
                     for i in range(NV):
-                        fills.append((EP, 0.5, lambda t=t, i=i: share_end(t, i)))
+                        for n in range(NA):
+                            fills.append((EP, 0.3, lambda t=t, i=i, n=n: share_op(t, i, n), "h"))
             elif e == "sq":
                 for i in range(NV):
                     fills.append((EP + i, 0.25, lambda i=i: share_quant(i)))
@@ -295,10 +290,6 @@ def tile_softmoedynamics_pa_kernel(tc, tokens, logits, W1, b1, g1, be1, out):
                 if fills[idx][0] <= e and (kind is None or fills[idx][-1] == kind):
                     run(idx)
 
-        for t in range(2):
-            for i in SHARE_POOL:
-                for n in range(NA):
-                    share_op(t, i, n)
 
         for g in range(G):
             ps = psH.tile([P, PACK, EP * GB], F32, tag="ph", name="ps%d" % g)
@@ -317,8 +308,8 @@ def tile_softmoedynamics_pa_kernel(tc, tokens, logits, W1, b1, g1, be1, out):
             afill(FRONT_CHUNKS[g])
             for w in range(FRONT_SHARE[g]):
                 fill(0.1)
-            if g in {1: 0, 4: 1, 9: 2}:
-                need({1: 0, 4: 1, 9: 2}[g], "w")
+            if g in {0: 1, 6: 2, 8: 3, 10: 4, 12: 5}:
+                need({0: 1, 6: 2, 8: 3, 10: 4, 12: 5}[g], "w")
         squant(0)
 
         xs, us, negmus, vss, rstds, mvs = {}, {}, {}, {}, {}, {}
@@ -327,7 +318,7 @@ def tile_softmoedynamics_pa_kernel(tc, tokens, logits, W1, b1, g1, be1, out):
 
         def mxa(e, t):
             if t == 0:
-                xs[e] = xp.tile([P, 2, H], F32, tag="x", name="x%d" % e)
+                xs[e] = big.tile([P, 2, H], F32, tag="big", name="x%d" % e, align_bytes=64)
                 negmus[e] = stp.tile([P, 2], F32, tag="negmu", name="negmu%d" % e)
             s01 = stp.tile([P, 2], F32, tag="s01", name="s01_%d_%d" % (e, t))
             for hh in range(2):
@@ -368,7 +359,7 @@ def tile_softmoedynamics_pa_kernel(tc, tokens, logits, W1, b1, g1, be1, out):
 
         def cc(e, t):
             if t == 0:
-                us[e] = up.tile([P, 2, H], F32, tag="u", name="u%d" % e)
+                us[e] = big.tile([P, 2, H], F32, tag="big", name="u%d" % e, align_bytes=64)
             if e in STATS_DVE:
                 nc.vector.scalar_tensor_tensor(
                     out=us[e][:, t, :], in0=xs[e][:, t, :], scalar=mvs[e][:, t, 0:1], in1=pgs[e][:],
@@ -395,6 +386,10 @@ def tile_softmoedynamics_pa_kernel(tc, tokens, logits, W1, b1, g1, be1, out):
         def rstd_of(k):
             lv = stp.tile([P, 2 * len(BATCHES[k])], F32, tag="lv", name="lv%d" % k)
             rstds[k] = stp.tile([P, 2 * len(BATCHES[k])], F32, tag="rstd", name="rstd%d" % k)
+            if RSTD_POOL:
+                nc.gpsimd.tensor_scalar(out=lv[:], in0=vss[k][:], scalar1=1.0 / H, scalar2=EPS, op0=ALU.mult, op1=ALU.add)
+                nc.gpsimd.tensor_tensor(out=rstds[k][:], in0=lv[:], in1=mhalf[:, 0:2 * len(BATCHES[k])], op=ALU.pow)
+                return
             for i in range(len(BATCHES[k])):
                 e = BATCHES[k][i]
                 if e in STATS_DVE:
@@ -453,20 +448,33 @@ def tile_softmoedynamics_pa_kernel(tc, tokens, logits, W1, b1, g1, be1, out):
         for c in range(-1, NB):
             prev = BATCHES[c] if c >= 0 else ()
             nxt = BATCHES[c + 1] if c + 1 < NB else ()
-            for i in range(max(len(prev), len(nxt))):
-                if i < len(prev):
-                    ln(prev[i])
-                if i < len(nxt):
+            if SQ_LATE and c >= 0:
+                for e in prev:
+                    ln(e)
+                for e in prev:
+                    fin(e)
+                for i in range(len(nxt)):
                     sq(c + 1, i)
-                    if c < 0:
-                        afill(PRO_CHUNKS[i])
-            if nxt:
-                rstd_of(c + 1)
-            fill(FILL1)
-            for i in range(len(nxt)):
-                dd(c + 1, i)
-            for e in prev:
-                fin(e)
+                if nxt:
+                    rstd_of(c + 1)
+                fill(FILL1)
+                for i in range(len(nxt)):
+                    dd(c + 1, i)
+            else:
+                for i in range(max(len(prev), len(nxt))):
+                    if i < len(prev):
+                        ln(prev[i])
+                    if i < len(nxt):
+                        sq(c + 1, i)
+                        if c < 0:
+                            afill(PRO_CHUNKS[i])
+                if nxt:
+                    rstd_of(c + 1)
+                fill(FILL1)
+                for i in range(len(nxt)):
+                    dd(c + 1, i)
+                for e in prev:
+                    fin(e)
             for e in nxt:
                 ex(e)
             if c < 0:

@@ -20,21 +20,9 @@ PACK = 4
 EPS = 1e-5
 EP = 6
 NV = E - EP
-CH = 256
-HV = (1024, 1024, 512, 512, 512, 512, 512, 512)
-BATCHES = ((0, 1), (2, 3), (4, 5), (6, 7))
-F_ON_POOL = (0, 1, 2, 3, 4)
-SPLIT_FIN = (6, 7)
-ACT_CASTS = (1, 2)
-FRONT_CHUNKS = (0, 0, 0, 0, 1, 1, 1, 1, 1, 1, 1, 1, 0, 0, 0, 0)
-FRONT_SHARE = (0, 0, 0, 0, 0, 0, 0, 0, 0, 0, 0, 0, 0, 0, 0, 0)
-PRO_CHUNKS = (2, 2, 0)
-FILL1, FILL3 = 0, 5
-SHARE_END_ACT = False
-NBIG = 10
-SQ_LATE = False
-RSTD_POOL = True
-STATS_DVE = ()
+NB = E // 2
+HS = 768
+POOL_BATCHES = 3
 
 FLOPS = 2 * E * B * D * H + 2 * B * NA * E * D
 
@@ -43,16 +31,16 @@ def tile_softmoedynamics_pa_kernel(tc, tokens, logits, W1, b1, g1, be1, out):
     nc = tc.nc
     with ExitStack() as ctx:
         cst = ctx.enter_context(tc.tile_pool(name="cst", bufs=1))
-        big = ctx.enter_context(tc.tile_pool(name="big", bufs=NBIG))
-        trp = ctx.enter_context(tc.tile_pool(name="trp", bufs=4))
-        wgp = ctx.enter_context(tc.tile_pool(name="wgp", bufs=3))
-        tnp = ctx.enter_context(tc.tile_pool(name="tnp", bufs=2))
-        wcp = ctx.enter_context(tc.tile_pool(name="wcp", bufs=E))
+        xp = ctx.enter_context(tc.tile_pool(name="xp", bufs=6))
+        up = ctx.enter_context(tc.tile_pool(name="up", bufs=6))
+        tnp = ctx.enter_context(tc.tile_pool(name="tnp", bufs=1))
+        wrp = ctx.enter_context(tc.tile_pool(name="wrp", bufs=3))
+        wgp = ctx.enter_context(tc.tile_pool(name="wgp", bufs=2))
+        wcp = ctx.enter_context(tc.tile_pool(name="wcp", bufs=5))
         bbp = ctx.enter_context(tc.tile_pool(name="bbp", bufs=3))
-        prp = ctx.enter_context(tc.tile_pool(name="prp", bufs=4))
+        acp = ctx.enter_context(tc.tile_pool(name="acp", bufs=1))
         stp = ctx.enter_context(tc.tile_pool(name="stp", bufs=8))
-        psH = ctx.enter_context(tc.psum_pool(name="psH", bufs=3))
-        psS = ctx.enter_context(tc.psum_pool(name="psS", bufs=1))
+        psH = ctx.enter_context(tc.psum_pool(name="psH", bufs=4))
         psG = ctx.enter_context(tc.psum_pool(name="psG", bufs=2))
         ctx.enter_context(tc.manual_schedule())
 
@@ -60,11 +48,8 @@ def tile_softmoedynamics_pa_kernel(tc, tokens, logits, W1, b1, g1, be1, out):
         make_identity(nc, ident[:])
         identb = cst.tile([P, P], BF16, name="identb")
         make_identity(nc, identb[:])
-        mhalf = cst.tile([P, 8], F32, name="mhalf")
+        mhalf = cst.tile([P, 4], F32, name="mhalf")
         nc.gpsimd.memset(mhalf[:], -0.5)
-        epst = cst.tile([P, 1], F32, name="epst")
-        nc.gpsimd.memset(epst[:], EPS)
-
         warm = cst.tile([P, 1], F32, name="warm")
         nc.vector.memset(warm[:], 0.0)
         nc.scalar.activation(out=warm[:], in_=warm[:], func=ACT.Exp)
@@ -79,50 +64,39 @@ def tile_softmoedynamics_pa_kernel(tc, tokens, logits, W1, b1, g1, be1, out):
         tok_view = tokens.rearrange("(g b) n d -> (b n) g d", b=GB)
         trs = []
         for q in range(4):
-            tr = trp.tile([P, 4, D], BF16, tag="tr", name="tr%d" % q)
+            tr = up.tile([P, 4, D], BF16, tag="u", name="tr%d" % q)
             nc.sync.dma_start(out=tr[:], in_=tok_view[:, 4 * q:4 * q + 4, :])
             trs.append(tr)
 
-        tfs = []
-        for q in range(4):
-            tf = big.tile([P, 4, D], F32, tag="big", name="tf%d" % q, align_bytes=64)
-            tfs.append(tf)
-        wrs, wgs, wcs, wss, bbs, tns = {}, {}, {}, {}, {}, {}
+        wrs, wcs, wss, bbs, tns = {}, {}, {}, {}, {}
 
-        def wload(e):
-            wr = big.tile([P, PACK, H], BF16, tag="big", name="wr%d" % e, align_bytes=64)
-            nc.sync.dma_start(out=wr[:], in_=W1[e].rearrange("(j p) h -> p j h", p=P))
-            wrs[e] = wr
+        def load_weights(e):
+            wrs[e] = wrp.tile([P, PACK, H], BF16, tag="wr", name="wr%d" % e)
+            nc.sync.dma_start(out=wrs[e][:], in_=W1[e].rearrange("(j p) h -> p j h", p=P))
 
-        def bload(e, eng):
-            bb = bbp.tile([P, H], BF16, tag="bb", name="bb%d" % e)
-            eng.dma_start(out=bb[:], in_=b1[e].partition_broadcast(P))
-            bbs[e] = bb
+        def load_bias(e, queue):
+            bbs[e] = bbp.tile([P, H], BF16, tag="bb", name="bb%d" % e)
+            queue.dma_start(out=bbs[e][:], in_=b1[e].partition_broadcast(P))
 
-        def tnload(t):
-            tn = tnp.tile([P, NA, D], BF16, tag="tn", name="tn%d" % t)
-            nc.sync.dma_start(out=tn[:], in_=tokens[P * t:P * t + P])
-            tns[t] = tn
+        def load_tokens_by_batch(t):
+            tns[t] = tnp.tile([P, NA, D], BF16, tag="tn", name="tn%d" % t)
+            nc.sync.dma_start(out=tns[t][:], in_=tokens[P * t:P * t + P])
 
-        for what in (0, 1, 2, 3, 4, 5):
-            if what >= 10:
-                tnload(what - 10)
-            else:
-                wload(what)
+        load_weights(0)
+        load_weights(1)
+        load_tokens_by_batch(0)
+        load_weights(2)
         for e in range(3):
-            bload(e, nc.gpsimd)
+            load_bias(e, nc.gpsimd)
 
         pgs, pbs = {}, {}
 
-        def peb(e):
-            pg = psG.tile([P, H], BF16, tag="pg", name="pg%d" % e)
-            pb = psG.tile([P, H], BF16, tag="pb", name="pb%d" % e)
-            for w, dst in ((0, pg), (1, pb)):
-                for c in range(8):
-                    col = 64 * w + 8 * e + c
-                    nc.tensor.transpose(dst[:, P * c:P * c + P], gcol[:, col:col + 1].to_broadcast([P, P]), identb[:])
-            pgs[e] = pg
-            pbs[e] = pb
+        def spread(w, e):
+            dst = psG.tile([P, H], BF16, tag="pg%d" % w, name="pg%d_%d" % (w, e))
+            for c in range(8):
+                col = 64 * w + 8 * e + c
+                nc.tensor.transpose(dst[:, P * c:P * c + P], gcol[:, col:col + 1].to_broadcast([P, P]), identb[:])
+            (pgs, pbs)[w][e] = dst
 
         mask = cst.tile([P, GB], F32, name="mask")
         nc.vector.tensor_reduce(out=mask[:], in_=ident[:].rearrange("p (b n) -> p b n", n=NA), axis=AX.X, op=ALU.add)
@@ -139,8 +113,9 @@ def tile_softmoedynamics_pa_kernel(tc, tokens, logits, W1, b1, g1, be1, out):
         nc.scalar.activation(out=sh[:], in_=sh[:], func=ACT.Exp)
         gcol = cst.tile([P, P], BF16, name="gcol")
         nc.vector.tensor_copy(out=gcol[:], in_=psR[:])
-        peb(0)
-        peb(1)
+        for e in range(2):
+            spread(0, e)
+            spread(1, e)
 
         dn = cst.tile([P, 2, NV, NA], F32, name="dn")
         dnv = dn[:].rearrange("b t e n -> b (t e) n")
@@ -163,12 +138,10 @@ def tile_softmoedynamics_pa_kernel(tc, tokens, logits, W1, b1, g1, be1, out):
         nc.vector.reciprocal(out=rsn[:], in_=smn[:])
         nc.vector.tensor_tensor(out=dnv, in0=dnv, in1=rsn[:].unsqueeze(2).to_broadcast([P, 2 * NV, NA]), op=ALU.mult)
 
-        def cast(q):
-            if q in ACT_CASTS:
-                nc.scalar.copy(out=tfs[q][:], in_=trs[q][:])
-            else:
-                nc.vector.tensor_copy(out=tfs[q][:], in_=trs[q][:])
-
+        tfs = []
+        for q in range(4):
+            tf = xp.tile([P, 4, D], F32, tag="x", name="tf%d" % q)
+            tfs.append(tf)
         dblk = cst.tile([P, G, EP, GB], F32, name="dblk")
         for g0 in (0, 8):
             nc.vector.tensor_tensor(
@@ -178,118 +151,55 @@ def tile_softmoedynamics_pa_kernel(tc, tokens, logits, W1, b1, g1, be1, out):
                 op=ALU.mult,
             )
             if g0 == 0:
-                cast(0)
+                nc.vector.tensor_copy(out=tfs[0][:], in_=trs[0][:])
         for q in range(1, 4):
-            cast(q)
-        for what in (6, 7, 10, 11):
-            if what >= 10:
-                tnload(what - 10)
-            else:
-                wload(what)
+            nc.scalar.copy(out=tfs[q][:], in_=trs[q][:])
 
-        def regroup(copy_fn, e, c0, c1):
-            if e not in wgs:
-                wgs[e] = wgp.tile([P, H, PACK], BF16, tag="wg", name="wg%d" % e, align_bytes=64)
-            copy_fn(
-                out=wgs[e][:, c0:c1, :].rearrange("p (c i) t -> p c t i", i=4),
-                in_=wrs[e][:, :, c0:c1].rearrange("p t (c i) -> p c t i", i=4),
-            )
-
-        achunks = [(e, c0) for e in range(E) for c0 in range(HV[e], H, CH)]
-        apos = [0]
-
-        def afill(n):
-            while n > 0 and apos[0] < len(achunks):
-                e, c0 = achunks[apos[0]]
-                apos[0] = apos[0] + 1
-                regroup(nc.scalar.copy, e, c0, c0 + CH)
-                n -= 1
-
-        def wquant(e):
-            while apos[0] < len(achunks) and achunks[apos[0]][0] <= e:
-                afill(1)
+        def prepare_weights(e):
+            wg = wgp.tile([P, H, PACK], BF16, tag="wg", name="wg%d" % e, align_bytes=64)
+            hs = HS
+            for copy_fn, c0, c1 in ((nc.vector.tensor_copy, 0, hs), (nc.scalar.copy, hs, H)):
+                if c1 > c0:
+                    copy_fn(
+                        out=wg[:, c0:c1, :].rearrange("p (c i) t -> p c t i", i=4),
+                        in_=wrs[e][:, :, c0:c1].rearrange("p t (c i) -> p c t i", i=4),
+                    )
             wcs[e] = wcp.tile([P, H], U32, tag="wc", name="wc%d" % e, align_bytes=64)
             wss[e] = wcp.tile([P, H], U8, tag="ws", name="ws%d" % e, align_bytes=64)
-            nc.vector.quantize_mx(
-                out=wcs[e][:].bitcast(FP8X4), scales=wss[e][:], in_=wgs[e][:].rearrange("p h j -> p (h j)")
-            )
+            nc.vector.quantize_mx(out=wcs[e][:].bitcast(FP8X4), scales=wss[e][:], in_=wg[:].rearrange("p h j -> p (h j)"))
+            if e + 3 < E:
+                load_weights(e + 3)
 
         gs = cst.tile([P, E, B, PACK], BF16, name="gs", align_bytes=64)
         sc = cst.tile([P, E, B], U32, name="sc", align_bytes=64)
         ss = cst.tile([P, E, B], U8, name="ss", align_bytes=64)
+
+        def quantise_slots(k):
+            nc.vector.quantize_mx(
+                out=sc[:, 2 * k:2 * k + 2, :].rearrange("p e b -> p (e b)").bitcast(FP8X4),
+                scales=ss[:, 2 * k:2 * k + 2, :].rearrange("p e b -> p (e b)"),
+                in_=gs[:, 2 * k:2 * k + 2, :, :].rearrange("p e b j -> p (e b j)"),
+            )
+
         accs = {}
 
-        def share_op(t, i, n):
-            pr = prp.tile([P, D], F32, tag="pr", name="pr%d_%d_%d" % (t, i, n))
-            nc.vector.tensor_scalar_mul(out=pr[:], in0=tns[t][:, n, :], scalar1=dn[:, t, i, n:n + 1])
-            if n == 0:
-                accs[(t, i)] = psS.tile([P, PACK, P], F32, tag="pss", name="pss%d_%d" % (t, i))
-            for j in range(PACK):
-                nc.tensor.matmul(
-                    accs[(t, i)][:, j, :],
-                    lhsT=pr[:, P * j:P * j + P],
-                    rhs=ident[:],
-                    is_transpose=True,
-                    start=(n == 0 and j == 0),
-                    stop=(n == NA - 1 and j == PACK - 1),
-                )
-            if n == NA - 1:
-                copy_fn = nc.scalar.copy if SHARE_END_ACT else nc.vector.tensor_copy
-                copy_fn(out=gs[:, EP + i, P * t:P * t + P, :], in_=accs[(t, i)][:].rearrange("p j b -> p b j"))
+        def sum_step(t, n):
+            for i in range(NV):
+                if n == 0:
+                    accs[i] = acp.tile([P, D], F32, tag="acc%d" % i, name="acc%d_%d" % (t, i))
+                    nc.vector.tensor_scalar_mul(out=accs[i][:], in0=tns[t][:, 0, :], scalar1=dn[:, t, i, 0:1])
+                else:
+                    nc.vector.scalar_tensor_tensor(
+                        out=accs[i][:], in0=tns[t][:, n, :], scalar=dn[:, t, i, n:n + 1], in1=accs[i][:],
+                        op0=ALU.mult, op1=ALU.add,
+                    )
 
-        def share_quant(i):
-            e = EP + i
-            nc.vector.quantize_mx(
-                out=sc[:, e, :].bitcast(FP8X4), scales=ss[:, e, :], in_=gs[:, e, :, :].rearrange("p b j -> p (b j)")
-            )
-
-        def squant(m):
-            nc.vector.quantize_mx(
-                out=sc[:, 2 * m:2 * m + 2, :].rearrange("p e b -> p (e b)").bitcast(FP8X4),
-                scales=ss[:, 2 * m:2 * m + 2, :].rearrange("p e b -> p (e b)"),
-                in_=gs[:, 2 * m:2 * m + 2, :, :].rearrange("p e b j -> p (e b j)"),
-            )
-
-        fills = []
-        order = (0, 1, 2, 3, 4, 5, "s1", 6, 7, "s2", "sh", "sq")
-        for e in order:
-            if e == "s1":
-                fills.append((2, 0.5, lambda: squant(1), "s"))
-            elif e == "s2":
-                fills.append((4, 0.5, lambda: squant(2), "s"))
-            elif e == "sh":
-                for t in range(2):
-                    for i in range(NV):
-                        for n in range(NA):
-                            fills.append((EP, 0.3, lambda t=t, i=i, n=n: share_op(t, i, n), "h"))
-            elif e == "sq":
-                for i in range(NV):
-                    fills.append((EP + i, 0.25, lambda i=i: share_quant(i)))
-            else:
-                for c0 in range(0, HV[e], 512):
-                    fills.append((e, 0.9, lambda e=e, c0=c0: regroup(nc.vector.tensor_copy, e, c0, min(c0 + 512, HV[e])), "w"))
-                fills.append((e, 0.9, lambda e=e: wquant(e), "w"))
-        pos = [0]
-        done = set()
-
-        def run(idx):
-            if idx not in done:
-                done.add(idx)
-                fills[idx][2]()
-
-        def fill(budget):
-            spent = 0.0
-            while pos[0] < len(fills) and spent < budget:
-                if pos[0] not in done:
-                    spent += fills[pos[0]][1]
-                run(pos[0])
-                pos[0] = pos[0] + 1
-
-        def need(e, kind=None):
-            for idx in range(len(fills)):
-                if fills[idx][0] <= e and (kind is None or fills[idx][-1] == kind):
-                    run(idx)
-
+        def sum_end(t):
+            for i in range(NV):
+                pst = psH.tile([P, PACK, P], F32, tag="ph", name="pst%d_%d" % (t, i))
+                for j in range(PACK):
+                    nc.tensor.transpose(pst[:, j, :], accs[i][:, P * j:P * j + P], ident[:])
+                nc.vector.tensor_copy(out=gs[:, EP + i, P * t:P * t + P, :], in_=pst[:].rearrange("p j b -> p b j"))
 
         for g in range(G):
             ps = psH.tile([P, PACK, EP * GB], F32, tag="ph", name="ps%d" % g)
@@ -301,127 +211,99 @@ def tile_softmoedynamics_pa_kernel(tc, tokens, logits, W1, b1, g1, be1, out):
                     start=True,
                     stop=True,
                 )
-            nc.scalar.copy(
-                out=gs[:, 0:EP, GB * g:GB * g + GB, :],
-                in_=ps[:].rearrange("p j (e b) -> p e b j", e=EP),
-            )
-            afill(FRONT_CHUNKS[g])
-            for w in range(FRONT_SHARE[g]):
-                fill(0.1)
-            if g in {0: 1, 6: 2, 8: 3, 10: 4, 12: 5}:
-                need({0: 1, 6: 2, 8: 3, 10: 4, 12: 5}[g], "w")
-        squant(0)
+            nc.scalar.copy(out=gs[:, 0:EP, GB * g:GB * g + GB, :], in_=ps[:].rearrange("p j (e b) -> p e b j", e=EP))
+            if g % 4 == 0:
+                prepare_weights(g // 4)
+            if 4 <= g < 4 + NA:
+                sum_step(0, g - 4)
+        load_tokens_by_batch(1)
+        quantise_slots(0)
 
-        xs, us, negmus, vss, rstds, mvs = {}, {}, {}, {}, {}, {}
+        xs, us, negmus, vss, rstds = {}, {}, {}, {}, {}
         junk = cst.tile([P, H], BF16, name="junk")
         out_v = out.rearrange("(t b) e h -> b t e h", b=P)
 
-        def mxa(e, t):
+        phs = {}
+
+        def multiply(e):
+            for t in range(2):
+                for hh in range(2):
+                    phs[(e, t, hh)] = psH.tile([P, 512], F32, tag="ph", name="ph%d_%d_%d" % (e, t, hh))
+                    nc.tensor.matmul_mx(
+                        out=phs[(e, t, hh)][:],
+                        lhsT=sc[:, e, P * t:P * t + P].bitcast(FP8X4),
+                        lhsT_scale=ss[:, e, P * t:P * t + P],
+                        rhs=wcs[e][:, 512 * hh:512 * hh + 512].bitcast(FP8X4),
+                        rhs_scale=wss[e][:, 512 * hh:512 * hh + 512],
+                        start=True,
+                        stop=True,
+                    )
+
+        def add_bias(e, t):
             if t == 0:
-                xs[e] = big.tile([P, 2, H], F32, tag="big", name="x%d" % e, align_bytes=64)
+                xs[e] = xp.tile([P, 2, H], F32, tag="x", name="x%d" % e)
                 negmus[e] = stp.tile([P, 2], F32, tag="negmu", name="negmu%d" % e)
             s01 = stp.tile([P, 2], F32, tag="s01", name="s01_%d_%d" % (e, t))
             for hh in range(2):
-                ph = psH.tile([P, 512], F32, tag="ph", name="ph%d_%d_%d" % (e, t, hh))
-                nc.tensor.matmul_mx(
-                    out=ph[:],
-                    lhsT=sc[:, e, P * t:P * t + P].bitcast(FP8X4),
-                    lhsT_scale=ss[:, e, P * t:P * t + P],
-                    rhs=wcs[e][:, 512 * hh:512 * hh + 512].bitcast(FP8X4),
-                    rhs_scale=wss[e][:, 512 * hh:512 * hh + 512],
-                    start=True,
-                    stop=True,
-                )
                 nc.vector.scalar_tensor_tensor(
                     out=xs[e][:, t, 512 * hh:512 * hh + 512],
-                    in0=ph[:],
+                    in0=phs[(e, t, hh)][:],
                     scalar=1.0,
                     in1=bbs[e][:, 512 * hh:512 * hh + 512],
                     op0=ALU.mult,
                     op1=ALU.add,
-                    accum_out=None if e in STATS_DVE else s01[:, hh:hh + 1],
+                    accum_out=s01[:, hh:hh + 1],
                 )
-            if e not in STATS_DVE:
-                nc.vector.tensor_scalar(
-                    out=negmus[e][:, t:t + 1], in0=s01[:, 0:1], scalar1=s01[:, 1:2], scalar2=-1.0 / H,
-                    op0=ALU.add, op1=ALU.mult,
-                )
+            nc.vector.tensor_scalar(
+                out=negmus[e][:, t:t + 1], in0=s01[:, 0:1], scalar1=s01[:, 1:2], scalar2=-1.0 / H,
+                op0=ALU.add, op1=ALU.mult,
+            )
             if t == 1 and e + 3 < E:
-                bload(e + 3, nc.sync)
+                load_bias(e + 3, nc.sync)
 
-        def bn(e, t):
-            if t == 0:
-                mvs[e] = stp.tile([P, 2, 2], F32, tag="mv", name="mv%d" % e)
-            st6 = stp.tile([P, 2, 6], F32, tag="st6", name="st6_%d_%d" % (e, t))
-            for hh in range(2):
-                nc.vector.bn_stats(out=st6[:, hh, :], in_=xs[e][:, t, 512 * hh:512 * hh + 512])
-            nc.vector.bn_aggr(out=mvs[e][:, t, :], in_=st6[:].rearrange("p a s -> p (a s)"))
-
-        def cc(e, t):
-            if t == 0:
-                us[e] = big.tile([P, 2, H], F32, tag="big", name="u%d" % e, align_bytes=64)
-            if e in STATS_DVE:
-                nc.vector.scalar_tensor_tensor(
-                    out=us[e][:, t, :], in0=xs[e][:, t, :], scalar=mvs[e][:, t, 0:1], in1=pgs[e][:],
-                    op0=ALU.subtract, op1=ALU.mult,
-                )
-            else:
+        def centre_times_gamma(e):
+            us[e] = up.tile([P, 2, H], F32, tag="u", name="u%d" % e)
+            for t in range(2):
                 nc.vector.scalar_tensor_tensor(
                     out=us[e][:, t, :], in0=xs[e][:, t, :], scalar=negmus[e][:, t:t + 1], in1=pgs[e][:],
                     op0=ALU.add, op1=ALU.mult,
                 )
+            if e + 2 < E:
+                spread(0, e + 2)
 
-        def sq(k, i):
-            e = BATCHES[k][i]
+        def sum_of_squares(k, i):
+            e = 2 * k + i
             if i == 0:
-                vss[k] = stp.tile([P, 2 * len(BATCHES[k])], F32, tag="vs", name="vs%d" % k)
+                vss[k] = stp.tile([P, 4], F32, tag="vs", name="vs%d" % k)
             for t in range(2):
-                if e in STATS_DVE:
-                    continue
                 nc.scalar.activation(
                     out=junk[:], in_=xs[e][:, t, :], func=ACT.Square, bias=negmus[e][:, t:t + 1],
                     accum_out=vss[k][:, 2 * i + t:2 * i + t + 1],
                 )
 
-        def rstd_of(k):
-            lv = stp.tile([P, 2 * len(BATCHES[k])], F32, tag="lv", name="lv%d" % k)
-            rstds[k] = stp.tile([P, 2 * len(BATCHES[k])], F32, tag="rstd", name="rstd%d" % k)
-            if RSTD_POOL:
-                nc.gpsimd.tensor_scalar(out=lv[:], in0=vss[k][:], scalar1=1.0 / H, scalar2=EPS, op0=ALU.mult, op1=ALU.add)
-                nc.gpsimd.tensor_tensor(out=rstds[k][:], in0=lv[:], in1=mhalf[:, 0:2 * len(BATCHES[k])], op=ALU.pow)
-                return
-            for i in range(len(BATCHES[k])):
-                e = BATCHES[k][i]
-                if e in STATS_DVE:
-                    nc.scalar.activation(out=lv[:, 2 * i:2 * i + 2], in_=mvs[e][:, :, 1], func=ACT.Ln, bias=epst[:])
-                else:
-                    nc.scalar.activation(
-                        out=lv[:, 2 * i:2 * i + 2], in_=vss[k][:, 2 * i:2 * i + 2], func=ACT.Ln, scale=1.0 / H, bias=epst[:]
-                    )
-            nc.scalar.activation(out=rstds[k][:], in_=lv[:], func=ACT.Exp, scale=-0.5)
+        def inverse_deviation(k):
+            ve = stp.tile([P, 4], F32, tag="ve", name="ve%d" % k)
+            rstds[k] = stp.tile([P, 4], F32, tag="rstd", name="rstd%d" % k)
+            nc.gpsimd.tensor_scalar(out=ve[:], in0=vss[k][:], scalar1=1.0 / H, scalar2=EPS, op0=ALU.mult, op1=ALU.add)
+            nc.gpsimd.tensor_tensor(out=rstds[k][:], in0=ve[:], in1=mhalf[:], op=ALU.pow)
 
-        def dd(k, i):
-            e = BATCHES[k][i]
+        def scale_add_beta(k, i):
+            e = 2 * k + i
             for t in range(2):
                 nc.vector.scalar_tensor_tensor(
                     out=xs[e][:, t, :], in0=us[e][:, t, :], scalar=rstds[k][:, 2 * i + t:2 * i + t + 1], in1=pbs[e][:],
                     op0=ALU.mult, op1=ALU.add,
                 )
             if e + 2 < E:
-                peb(e + 2)
+                spread(1, e + 2)
 
         def flat(tl):
             return tl[:].rearrange("p t h -> p (t h)")
 
-        def ex(e):
-            nc.scalar.activation(out=flat(us[e]), in_=flat(xs[e]), func=ACT.Exp)
-
-        def ln(e):
-            nc.scalar.activation(out=flat(us[e]), in_=flat(us[e]), func=ACT.Ln, bias=1.0)
-
-        def fin(e):
-            eng = nc.gpsimd if e in F_ON_POOL else nc.vector
-            if e not in SPLIT_FIN:
+        def finish(k, i):
+            e = 2 * k + i
+            eng = nc.gpsimd if k < POOL_BATCHES else nc.vector
+            if k < NB - 1:
                 nc.scalar.activation(out=flat(us[e]), in_=flat(us[e]), func=ACT.Tanh)
                 for t in range(2):
                     eng.tensor_tensor(out=us[e][:, t, :], in0=xs[e][:, t, :], in1=us[e][:, t, :], op=ALU.mult)
@@ -433,52 +315,47 @@ def tile_softmoedynamics_pa_kernel(tc, tokens, logits, W1, b1, g1, be1, out):
                     nc.sync.dma_start(out=out_v[:, t, e, :], in_=us[e][:, t, :])
 
         def head(k):
-            need(max(BATCHES[k]))
-            for e in BATCHES[k]:
-                mxa(e, 0)
-                mxa(e, 1)
-                if e in STATS_DVE:
-                    bn(e, 0)
-                    bn(e, 1)
-                cc(e, 0)
-                cc(e, 1)
+            add_bias(2 * k, 0)
+            add_bias(2 * k, 1)
+            multiply(2 * k + 1)
+            centre_times_gamma(2 * k)
+            add_bias(2 * k + 1, 0)
+            add_bias(2 * k + 1, 1)
+            centre_times_gamma(2 * k + 1)
 
-        NB = len(BATCHES)
+        multiply(0)
         head(0)
+        quantise_slots(1)
         for c in range(-1, NB):
-            prev = BATCHES[c] if c >= 0 else ()
-            nxt = BATCHES[c + 1] if c + 1 < NB else ()
-            if SQ_LATE and c >= 0:
-                for e in prev:
-                    ln(e)
-                for e in prev:
-                    fin(e)
-                for i in range(len(nxt)):
-                    sq(c + 1, i)
-                if nxt:
-                    rstd_of(c + 1)
-                fill(FILL1)
-                for i in range(len(nxt)):
-                    dd(c + 1, i)
-            else:
-                for i in range(max(len(prev), len(nxt))):
-                    if i < len(prev):
-                        ln(prev[i])
-                    if i < len(nxt):
-                        sq(c + 1, i)
-                        if c < 0:
-                            afill(PRO_CHUNKS[i])
-                if nxt:
-                    rstd_of(c + 1)
-                fill(FILL1)
-                for i in range(len(nxt)):
-                    dd(c + 1, i)
-                for e in prev:
-                    fin(e)
-            for e in nxt:
-                ex(e)
-            if c < 0:
-                afill(PRO_CHUNKS[2])
+            if c + 2 < NB:
+                multiply(2 * (c + 2))
+            for i in range(2):
+                if c >= 0:
+                    nc.scalar.activation(out=flat(us[2 * c + i]), in_=flat(us[2 * c + i]), func=ACT.Ln, bias=1.0)
+                if c + 1 < NB:
+                    sum_of_squares(c + 1, i)
+            if c + 1 < NB:
+                inverse_deviation(c + 1)
+                for i in range(2):
+                    scale_add_beta(c + 1, i)
+            if c >= 0:
+                for i in range(2):
+                    finish(c, i)
+            if c + 1 < NB:
+                for i in range(2):
+                    e = 2 * (c + 1) + i
+                    nc.scalar.activation(out=flat(us[e]), in_=flat(xs[e]), func=ACT.Exp)
             if c + 2 < NB:
                 head(c + 2)
-            fill(FILL3)
+            if c + 3 < NB:
+                prepare_weights(2 * (c + 3))
+                prepare_weights(2 * (c + 3) + 1)
+            if c == -1:
+                quantise_slots(2)
+                sum_end(0)
+            if c in (-1, 0):
+                for n in range(4 * (c + 1), 4 * (c + 1) + 4):
+                    sum_step(1, n)
+            if c == 0:
+                sum_end(1)
+                quantise_slots(3)

@@ -22,6 +22,7 @@ EP = 6
 NV = E - EP
 NB = E // 2
 HS = 768
+VECTOR_STATS_FROM = 3
 POOL_BATCHES = 3
 
 FLOPS = 2 * E * B * D * H + 2 * B * NA * E * D
@@ -37,7 +38,6 @@ def tile_softmoedynamics_pa_kernel(tc, tokens, logits, W1, b1, g1, be1, out):
         wrp = ctx.enter_context(tc.tile_pool(name="wrp", bufs=3))
         wgp = ctx.enter_context(tc.tile_pool(name="wgp", bufs=2))
         wcp = ctx.enter_context(tc.tile_pool(name="wcp", bufs=5))
-        bbp = ctx.enter_context(tc.tile_pool(name="bbp", bufs=3))
         acp = ctx.enter_context(tc.tile_pool(name="acp", bufs=1))
         stp = ctx.enter_context(tc.tile_pool(name="stp", bufs=8))
         psH = ctx.enter_context(tc.psum_pool(name="psH", bufs=4))
@@ -68,15 +68,19 @@ def tile_softmoedynamics_pa_kernel(tc, tokens, logits, W1, b1, g1, be1, out):
             nc.sync.dma_start(out=tr[:], in_=tok_view[:, 4 * q:4 * q + 4, :])
             trs.append(tr)
 
-        wrs, wcs, wss, bbs, tns = {}, {}, {}, {}, {}
+        wrs, wcs, wss, tns = {}, {}, {}, {}
 
         def load_weights(e):
             wrs[e] = wrp.tile([P, PACK, H], BF16, tag="wr", name="wr%d" % e)
             nc.sync.dma_start(out=wrs[e][:], in_=W1[e].rearrange("(j p) h -> p j h", p=P))
 
-        def load_bias(e, queue):
-            bbs[e] = bbp.tile([P, H], BF16, tag="bb", name="bb%d" % e)
-            queue.dma_start(out=bbs[e][:], in_=b1[e].partition_broadcast(P))
+        bb = cst.tile([P, E, H], BF16, name="bb")
+
+        def load_bias(half):
+            nc.sync.dma_start(
+                out=bb[:, 4 * half:4 * half + 4, :].rearrange("p e h -> p (e h)"),
+                in_=b1[4 * half:4 * half + 4].rearrange("e h -> (e h)").partition_broadcast(P),
+            )
 
         def load_tokens_by_batch(t):
             tns[t] = tnp.tile([P, NA, D], BF16, tag="tn", name="tn%d" % t)
@@ -85,9 +89,8 @@ def tile_softmoedynamics_pa_kernel(tc, tokens, logits, W1, b1, g1, be1, out):
         load_weights(0)
         load_weights(1)
         load_tokens_by_batch(0)
+        load_bias(0)
         load_weights(2)
-        for e in range(3):
-            load_bias(e, nc.gpsimd)
 
         pgs, pbs = {}, {}
 
@@ -217,9 +220,10 @@ def tile_softmoedynamics_pa_kernel(tc, tokens, logits, W1, b1, g1, be1, out):
             if 4 <= g < 4 + NA:
                 sum_step(0, g - 4)
         load_tokens_by_batch(1)
+        load_bias(1)
         quantise_slots(0)
 
-        xs, us, negmus, vss, rstds = {}, {}, {}, {}, {}
+        xs, us, negmus, vss, rstds, mvs = {}, {}, {}, {}, {}, {}
         junk = cst.tile([P, H], BF16, name="junk")
         out_v = out.rearrange("(t b) e h -> b t e h", b=P)
 
@@ -249,7 +253,7 @@ def tile_softmoedynamics_pa_kernel(tc, tokens, logits, W1, b1, g1, be1, out):
                     out=xs[e][:, t, 512 * hh:512 * hh + 512],
                     in0=phs[(e, t, hh)][:],
                     scalar=1.0,
-                    in1=bbs[e][:, 512 * hh:512 * hh + 512],
+                    in1=bb[:, e, 512 * hh:512 * hh + 512],
                     op0=ALU.mult,
                     op1=ALU.add,
                     accum_out=s01[:, hh:hh + 1],
@@ -258,8 +262,13 @@ def tile_softmoedynamics_pa_kernel(tc, tokens, logits, W1, b1, g1, be1, out):
                 out=negmus[e][:, t:t + 1], in0=s01[:, 0:1], scalar1=s01[:, 1:2], scalar2=-1.0 / H,
                 op0=ALU.add, op1=ALU.mult,
             )
-            if t == 1 and e + 3 < E:
-                load_bias(e + 3, nc.sync)
+            if e // 2 >= VECTOR_STATS_FROM:
+                if e % 2 == 0 and t == 0:
+                    mvs[e // 2] = stp.tile([P, 4, 2], F32, tag="mv", name="mv%d" % (e // 2))
+                st6 = stp.tile([P, 2, 6], F32, tag="st6", name="st6_%d_%d" % (e, t))
+                for hh in range(2):
+                    nc.vector.bn_stats(out=st6[:, hh, :], in_=xs[e][:, t, 512 * hh:512 * hh + 512])
+                nc.vector.bn_aggr(out=mvs[e // 2][:, 2 * (e % 2) + t, :], in_=st6[:].rearrange("p a s -> p (a s)"))
 
         def centre_times_gamma(e):
             us[e] = up.tile([P, 2, H], F32, tag="u", name="u%d" % e)
@@ -273,6 +282,8 @@ def tile_softmoedynamics_pa_kernel(tc, tokens, logits, W1, b1, g1, be1, out):
 
         def sum_of_squares(k, i):
             e = 2 * k + i
+            if k >= VECTOR_STATS_FROM:
+                return
             if i == 0:
                 vss[k] = stp.tile([P, 4], F32, tag="vs", name="vs%d" % k)
             for t in range(2):
@@ -284,7 +295,10 @@ def tile_softmoedynamics_pa_kernel(tc, tokens, logits, W1, b1, g1, be1, out):
         def inverse_deviation(k):
             ve = stp.tile([P, 4], F32, tag="ve", name="ve%d" % k)
             rstds[k] = stp.tile([P, 4], F32, tag="rstd", name="rstd%d" % k)
-            nc.gpsimd.tensor_scalar(out=ve[:], in0=vss[k][:], scalar1=1.0 / H, scalar2=EPS, op0=ALU.mult, op1=ALU.add)
+            if k >= VECTOR_STATS_FROM:
+                nc.gpsimd.tensor_scalar(out=ve[:], in0=mvs[k][:, :, 1], scalar1=1.0, scalar2=EPS, op0=ALU.mult, op1=ALU.add)
+            else:
+                nc.gpsimd.tensor_scalar(out=ve[:], in0=vss[k][:], scalar1=1.0 / H, scalar2=EPS, op0=ALU.mult, op1=ALU.add)
             nc.gpsimd.tensor_tensor(out=rstds[k][:], in0=ve[:], in1=mhalf[:], op=ALU.pow)
 
         def scale_add_beta(k, i):

@@ -22,6 +22,7 @@ EP = 6
 NV = E - EP
 NB = E // 2
 HS = 768
+HS_LATE = 512
 VECTOR_STATS_FROM = 3
 POOL_BATCHES = 3
 
@@ -89,7 +90,6 @@ def tile_softmoedynamics_pa_kernel(tc, tokens, logits, W1, b1, g1, be1, out):
         load_weights(0)
         load_weights(1)
         load_tokens_by_batch(0)
-        load_bias(0)
         load_weights(2)
 
         pgs, pbs = {}, {}
@@ -158,20 +158,25 @@ def tile_softmoedynamics_pa_kernel(tc, tokens, logits, W1, b1, g1, be1, out):
         for q in range(1, 4):
             nc.scalar.copy(out=tfs[q][:], in_=trs[q][:])
 
-        def prepare_weights(e):
-            wg = wgp.tile([P, H, PACK], BF16, tag="wg", name="wg%d" % e, align_bytes=64)
-            hs = HS
+        wgs = {}
+
+        def regroup(e):
+            wgs[e] = wgp.tile([P, H, PACK], BF16, tag="wg", name="wg%d" % e, align_bytes=64)
+            hs = HS if e < 4 else HS_LATE
             for copy_fn, c0, c1 in ((nc.vector.tensor_copy, 0, hs), (nc.scalar.copy, hs, H)):
-                if c1 > c0:
-                    copy_fn(
-                        out=wg[:, c0:c1, :].rearrange("p (c i) t -> p c t i", i=4),
-                        in_=wrs[e][:, :, c0:c1].rearrange("p t (c i) -> p c t i", i=4),
-                    )
-            wcs[e] = wcp.tile([P, H], U32, tag="wc", name="wc%d" % e, align_bytes=64)
-            wss[e] = wcp.tile([P, H], U8, tag="ws", name="ws%d" % e, align_bytes=64)
-            nc.vector.quantize_mx(out=wcs[e][:].bitcast(FP8X4), scales=wss[e][:], in_=wg[:].rearrange("p h j -> p (h j)"))
+                copy_fn(
+                    out=wgs[e][:, c0:c1, :].rearrange("p (c i) t -> p c t i", i=4),
+                    in_=wrs[e][:, :, c0:c1].rearrange("p t (c i) -> p c t i", i=4),
+                )
             if e + 3 < E:
                 load_weights(e + 3)
+
+        def quantise_weights(e):
+            wcs[e] = wcp.tile([P, H], U32, tag="wc", name="wc%d" % e, align_bytes=64)
+            wss[e] = wcp.tile([P, H], U8, tag="ws", name="ws%d" % e, align_bytes=64)
+            nc.vector.quantize_mx(
+                out=wcs[e][:].bitcast(FP8X4), scales=wss[e][:], in_=wgs[e][:].rearrange("p h j -> p (h j)")
+            )
 
         gs = cst.tile([P, E, B, PACK], BF16, name="gs", align_bytes=64)
         sc = cst.tile([P, E, B], U32, name="sc", align_bytes=64)
@@ -197,12 +202,17 @@ def tile_softmoedynamics_pa_kernel(tc, tokens, logits, W1, b1, g1, be1, out):
                         op0=ALU.mult, op1=ALU.add,
                     )
 
-        def sum_end(t):
+        psts = {}
+
+        def sum_transpose(t):
             for i in range(NV):
-                pst = psH.tile([P, PACK, P], F32, tag="ph", name="pst%d_%d" % (t, i))
+                psts[i] = psH.tile([P, PACK, P], F32, tag="ph", name="pst%d_%d" % (t, i))
                 for j in range(PACK):
-                    nc.tensor.transpose(pst[:, j, :], accs[i][:, P * j:P * j + P], ident[:])
-                nc.vector.tensor_copy(out=gs[:, EP + i, P * t:P * t + P, :], in_=pst[:].rearrange("p j b -> p b j"))
+                    nc.tensor.transpose(psts[i][:, j, :], accs[i][:, P * j:P * j + P], ident[:])
+
+        def sum_store(t):
+            for i in range(NV):
+                nc.vector.tensor_copy(out=gs[:, EP + i, P * t:P * t + P, :], in_=psts[i][:].rearrange("p j b -> p b j"))
 
         for g in range(G):
             ps = psH.tile([P, PACK, EP * GB], F32, tag="ph", name="ps%d" % g)
@@ -216,11 +226,14 @@ def tile_softmoedynamics_pa_kernel(tc, tokens, logits, W1, b1, g1, be1, out):
                 )
             nc.scalar.copy(out=gs[:, 0:EP, GB * g:GB * g + GB, :], in_=ps[:].rearrange("p j (e b) -> p e b j", e=EP))
             if g % 4 == 0:
-                prepare_weights(g // 4)
+                regroup(g // 4)
+            if g % 4 == 2:
+                quantise_weights(g // 4)
+            if g % 8 == 4:
+                load_bias(g // 8)
             if 4 <= g < 4 + NA:
                 sum_step(0, g - 4)
         load_tokens_by_batch(1)
-        load_bias(1)
         quantise_slots(0)
 
         xs, us, negmus, vss, rstds, mvs = {}, {}, {}, {}, {}, {}
@@ -244,10 +257,13 @@ def tile_softmoedynamics_pa_kernel(tc, tokens, logits, W1, b1, g1, be1, out):
                     )
 
         def add_bias(e, t):
+            by_vector = e // 2 >= VECTOR_STATS_FROM
             if t == 0:
                 xs[e] = xp.tile([P, 2, H], F32, tag="x", name="x%d" % e)
+            if t == 0 and not by_vector:
                 negmus[e] = stp.tile([P, 2], F32, tag="negmu", name="negmu%d" % e)
-            s01 = stp.tile([P, 2], F32, tag="s01", name="s01_%d_%d" % (e, t))
+            if not by_vector:
+                s01 = stp.tile([P, 2], F32, tag="s01", name="s01_%d_%d" % (e, t))
             for hh in range(2):
                 nc.vector.scalar_tensor_tensor(
                     out=xs[e][:, t, 512 * hh:512 * hh + 512],
@@ -256,13 +272,14 @@ def tile_softmoedynamics_pa_kernel(tc, tokens, logits, W1, b1, g1, be1, out):
                     in1=bb[:, e, 512 * hh:512 * hh + 512],
                     op0=ALU.mult,
                     op1=ALU.add,
-                    accum_out=s01[:, hh:hh + 1],
+                    accum_out=None if by_vector else s01[:, hh:hh + 1],
                 )
-            nc.vector.tensor_scalar(
-                out=negmus[e][:, t:t + 1], in0=s01[:, 0:1], scalar1=s01[:, 1:2], scalar2=-1.0 / H,
-                op0=ALU.add, op1=ALU.mult,
-            )
-            if e // 2 >= VECTOR_STATS_FROM:
+            if not by_vector:
+                nc.vector.tensor_scalar(
+                    out=negmus[e][:, t:t + 1], in0=s01[:, 0:1], scalar1=s01[:, 1:2], scalar2=-1.0 / H,
+                    op0=ALU.add, op1=ALU.mult,
+                )
+            else:
                 if e % 2 == 0 and t == 0:
                     mvs[e // 2] = stp.tile([P, 4, 2], F32, tag="mv", name="mv%d" % (e // 2))
                 st6 = stp.tile([P, 2, 6], F32, tag="st6", name="st6_%d_%d" % (e, t))
@@ -273,10 +290,16 @@ def tile_softmoedynamics_pa_kernel(tc, tokens, logits, W1, b1, g1, be1, out):
         def centre_times_gamma(e):
             us[e] = up.tile([P, 2, H], F32, tag="u", name="u%d" % e)
             for t in range(2):
-                nc.vector.scalar_tensor_tensor(
-                    out=us[e][:, t, :], in0=xs[e][:, t, :], scalar=negmus[e][:, t:t + 1], in1=pgs[e][:],
-                    op0=ALU.add, op1=ALU.mult,
-                )
+                if e // 2 >= VECTOR_STATS_FROM:
+                    nc.vector.scalar_tensor_tensor(
+                        out=us[e][:, t, :], in0=xs[e][:, t, :], scalar=mvs[e // 2][:, 2 * (e % 2) + t, 0:1], in1=pgs[e][:],
+                        op0=ALU.subtract, op1=ALU.mult,
+                    )
+                else:
+                    nc.vector.scalar_tensor_tensor(
+                        out=us[e][:, t, :], in0=xs[e][:, t, :], scalar=negmus[e][:, t:t + 1], in1=pgs[e][:],
+                        op0=ALU.add, op1=ALU.mult,
+                    )
             if e + 2 < E:
                 spread(0, e + 2)
 
@@ -362,14 +385,19 @@ def tile_softmoedynamics_pa_kernel(tc, tokens, logits, W1, b1, g1, be1, out):
             if c + 2 < NB:
                 head(c + 2)
             if c + 3 < NB:
-                prepare_weights(2 * (c + 3))
-                prepare_weights(2 * (c + 3) + 1)
-            if c == -1:
-                quantise_slots(2)
-                sum_end(0)
-            if c in (-1, 0):
+                if c == -1:
+                    sum_transpose(0)
+                regroup(2 * (c + 3))
+                regroup(2 * (c + 3) + 1)
+                if c == -1:
+                    quantise_slots(2)
+                    sum_store(0)
                 for n in range(4 * (c + 1), 4 * (c + 1) + 4):
                     sum_step(1, n)
-            if c == 0:
-                sum_end(1)
-                quantise_slots(3)
+                if c == 0:
+                    sum_transpose(1)
+                quantise_weights(2 * (c + 3))
+                quantise_weights(2 * (c + 3) + 1)
+                if c == 0:
+                    sum_store(1)
+                    quantise_slots(3)

@@ -24,7 +24,7 @@ NB = E // 2
 HS = 768
 HS_LATE = 512
 VECTOR_STATS_FROM = 3
-POOL_BATCHES = 3
+POOL_BATCHES = 2
 
 FLOPS = 2 * E * B * D * H + 2 * B * NA * E * D
 

@@ -24,7 +24,7 @@ NB = E // 2
 HS = 768
 HS_LATE = 512
 VECTOR_STATS_FROM = 3
-POOL_BATCHES = 2
+POOL_BATCHES = 3
 
 FLOPS = 2 * E * B * D * H + 2 * B * NA * E * D
 
@@ -43,7 +43,6 @@ def tile_softmoedynamics_pa_kernel(tc, tokens, logits, W1, b1, g1, be1, out):
         stp = ctx.enter_context(tc.tile_pool(name="stp", bufs=8))
         psH = ctx.enter_context(tc.psum_pool(name="psH", bufs=4))
         psG = ctx.enter_context(tc.psum_pool(name="psG", bufs=2))
-        ctx.enter_context(tc.manual_schedule())
 
         ident = cst.tile([P, P], F32, name="ident")
         make_identity(nc, ident[:])

from contextlib import ExitStack

import concourse.mybir as mybir
from concourse.masks import make_identity

F32 = mybir.dt.float32
BF16 = mybir.dt.bfloat16
U32 = mybir.dt.uint32
U8 = mybir.dt.uint8
FP8X4 = mybir.dt.float8_e4m3fn_x4
ALU = mybir.AluOpType
ACT = mybir.ActivationFunctionType
AX = mybir.AxisListType

P = 128
B, NA, E, D, H = 256, 8, 8, 512, 1024
G = 16
GB = 16
PACK = 4
EPS = 1e-5
EP = 6
NV = E - EP
NB = E // 2
HS = 768
HS_LATE = 512
VECTOR_STATS_FROM = 3
POOL_BATCHES = 3

FLOPS = 2 * E * B * D * H + 2 * B * NA * E * D


def tile_softmoedynamics_pa_kernel(tc, tokens, logits, W1, b1, g1, be1, out):
    nc = tc.nc
    with ExitStack() as ctx:
        cst = ctx.enter_context(tc.tile_pool(name="cst", bufs=1))
        xp = ctx.enter_context(tc.tile_pool(name="xp", bufs=6))
        up = ctx.enter_context(tc.tile_pool(name="up", bufs=6))
        tnp = ctx.enter_context(tc.tile_pool(name="tnp", bufs=1))
        wrp = ctx.enter_context(tc.tile_pool(name="wrp", bufs=3))
        wgp = ctx.enter_context(tc.tile_pool(name="wgp", bufs=2))
        wcp = ctx.enter_context(tc.tile_pool(name="wcp", bufs=5))
        acp = ctx.enter_context(tc.tile_pool(name="acp", bufs=1))
        stp = ctx.enter_context(tc.tile_pool(name="stp", bufs=8))
        psH = ctx.enter_context(tc.psum_pool(name="psH", bufs=4))
        psG = ctx.enter_context(tc.psum_pool(name="psG", bufs=2))

        ident = cst.tile([P, P], F32, name="ident")
        make_identity(nc, ident[:])
        identb = cst.tile([P, P], BF16, name="identb")
        make_identity(nc, identb[:])
        mhalf = cst.tile([P, 4], F32, name="mhalf")
        nc.gpsimd.memset(mhalf[:], -0.5)
        warm = cst.tile([P, 1], F32, name="warm")
        nc.vector.memset(warm[:], 0.0)
        nc.scalar.activation(out=warm[:], in_=warm[:], func=ACT.Exp)

        lg_raw = cst.tile([P, G, 16], BF16, name="lg_raw")
        nc.sync.dma_start(out=lg_raw[:, :, 0:E], in_=logits.rearrange("(g b) n e -> (b n) g e", b=GB))
        rows = cst.tile([P, P], BF16, name="rows")
        nc.sync.dma_start(out=rows[0:64, :], in_=g1.rearrange("e (c q) -> (e c) q", q=P))
        nc.sync.dma_start(out=rows[64:128, :], in_=be1.rearrange("e (c q) -> (e c) q", q=P))
        lgn = cst.tile([P, 2, NA * E], BF16, name="lgn")
        nc.sync.dma_start(out=lgn[:], in_=logits.rearrange("(t b) n e -> b t (n e)", b=P))
        tok_view = tokens.rearrange("(g b) n d -> (b n) g d", b=GB)
        trs = []
        for q in range(4):
            tr = up.tile([P, 4, D], BF16, tag="u", name="tr%d" % q)
            nc.sync.dma_start(out=tr[:], in_=tok_view[:, 4 * q:4 * q + 4, :])
            trs.append(tr)

        wrs, wcs, wss, tns = {}, {}, {}, {}

        def load_weights(e):
            wrs[e] = wrp.tile([P, PACK, H], BF16, tag="wr", name="wr%d" % e)
            nc.sync.dma_start(out=wrs[e][:], in_=W1[e].rearrange("(j p) h -> p j h", p=P))

        bb = cst.tile([P, E, H], BF16, name="bb")

        def load_bias(half):
            nc.sync.dma_start(
                out=bb[:, 4 * half:4 * half + 4, :].rearrange("p e h -> p (e h)"),
                in_=b1[4 * half:4 * half + 4].rearrange("e h -> (e h)").partition_broadcast(P),
            )

        def load_tokens_by_batch(t):
            tns[t] = tnp.tile([P, NA, D], BF16, tag="tn", name="tn%d" % t)
            nc.sync.dma_start(out=tns[t][:], in_=tokens[P * t:P * t + P])

        load_weights(0)
        load_weights(1)
        load_tokens_by_batch(0)
        load_weights(2)

        pgs, pbs = {}, {}

        def spread(w, e):
            dst = psG.tile([P, H], BF16, tag="pg%d" % w, name="pg%d_%d" % (w, e))
            for c in range(8):
                col = 64 * w + 8 * e + c
                nc.tensor.transpose(dst[:, P * c:P * c + P], gcol[:, col:col + 1].to_broadcast([P, P]), identb[:])
            (pgs, pbs)[w][e] = dst

        mask = cst.tile([P, GB], F32, name="mask")
        nc.vector.tensor_reduce(out=mask[:], in_=ident[:].rearrange("p (b n) -> p b n", n=NA), axis=AX.X, op=ALU.add)
        lgf = cst.tile([P, G, E], F32, name="lgf")
        nc.vector.tensor_copy(out=lgf[:], in_=lg_raw[:, :, 0:E])
        psT = psH.tile([P, GB, NA], F32, tag="ph", name="psT")
        nc.tensor.transpose(psT[:].rearrange("p b n -> p (b n)"), lgf[:].rearrange("p g e -> p (g e)"), ident[:])
        psR = psH.tile([P, P], BF16, tag="ph", name="psR")
        nc.tensor.transpose(psR[:], rows[:], identb[:])
        mx = cst.tile([P, GB], F32, name="mx")
        nc.vector.tensor_reduce(out=mx[:], in_=psT[:], axis=AX.X, op=ALU.max)
        sh = cst.tile([P, GB, NA], F32, name="sh")
        nc.vector.tensor_tensor(out=sh[:], in0=psT[:], in1=mx[:].unsqueeze(2).to_broadcast([P, GB, NA]), op=ALU.subtract)
        nc.scalar.activation(out=sh[:], in_=sh[:], func=ACT.Exp)
        gcol = cst.tile([P, P], BF16, name="gcol")
        nc.vector.tensor_copy(out=gcol[:], in_=psR[:])
        for e in range(2):
            spread(0, e)
            spread(1, e)

        dn = cst.tile([P, 2, NV, NA], F32, name="dn")
        dnv = dn[:].rearrange("b t e n -> b (t e) n")
        nc.vector.tensor_copy(out=dn[:], in_=lgn[:].rearrange("b t (n e) -> b t e n", e=E)[:, :, EP:E, :])
        mxn = cst.tile([P, 2 * NV], F32, name="mxn")
        nc.vector.tensor_reduce(out=mxn[:], in_=dnv, axis=AX.X, op=ALU.max)
        nc.vector.tensor_tensor(out=dnv, in0=dnv, in1=mxn[:].unsqueeze(2).to_broadcast([P, 2 * NV, NA]), op=ALU.subtract)
        nc.scalar.activation(out=dnv, in_=dnv, func=ACT.Exp)

        sm = cst.tile([P, GB], F32, name="sm")
        nc.vector.tensor_reduce(out=sm[:], in_=sh[:], axis=AX.X, op=ALU.add)
        rs = cst.tile([P, GB], F32, name="rs")
        nc.vector.reciprocal(out=rs[:], in_=sm[:])
        nc.vector.tensor_tensor(out=sh[:], in0=sh[:], in1=rs[:].unsqueeze(2).to_broadcast([P, GB, NA]), op=ALU.mult)
        psD = psH.tile([P, G, E], F32, tag="ph", name="psD")
        nc.tensor.transpose(psD[:].rearrange("p g e -> p (g e)"), sh[:].rearrange("p b n -> p (b n)"), ident[:])
        smn = cst.tile([P, 2 * NV], F32, name="smn")
        nc.vector.tensor_reduce(out=smn[:], in_=dnv, axis=AX.X, op=ALU.add)
        rsn = cst.tile([P, 2 * NV], F32, name="rsn")
        nc.vector.reciprocal(out=rsn[:], in_=smn[:])
        nc.vector.tensor_tensor(out=dnv, in0=dnv, in1=rsn[:].unsqueeze(2).to_broadcast([P, 2 * NV, NA]), op=ALU.mult)

        tfs = []
        for q in range(4):
            tf = xp.tile([P, 4, D], F32, tag="x", name="tf%d" % q)
            tfs.append(tf)
        dblk = cst.tile([P, G, EP, GB], F32, name="dblk")
        for g0 in (0, 8):
            nc.vector.tensor_tensor(
                out=dblk[:, g0:g0 + 8, :, :],
                in0=psD[:, g0:g0 + 8, 0:EP].unsqueeze(3).to_broadcast([P, 8, EP, GB]),
                in1=mask[:].unsqueeze(1).unsqueeze(1).to_broadcast([P, 8, EP, GB]),
                op=ALU.mult,
            )
            if g0 == 0:
                nc.vector.tensor_copy(out=tfs[0][:], in_=trs[0][:])
        for q in range(1, 4):
            nc.scalar.copy(out=tfs[q][:], in_=trs[q][:])

        wgs = {}

        def regroup(e):
            wgs[e] = wgp.tile([P, H, PACK], BF16, tag="wg", name="wg%d" % e, align_bytes=64)
            hs = HS if e < 4 else HS_LATE
            for copy_fn, c0, c1 in ((nc.vector.tensor_copy, 0, hs), (nc.scalar.copy, hs, H)):
                copy_fn(
                    out=wgs[e][:, c0:c1, :].rearrange("p (c i) t -> p c t i", i=4),
                    in_=wrs[e][:, :, c0:c1].rearrange("p t (c i) -> p c t i", i=4),
                )
            if e + 3 < E:
                load_weights(e + 3)

        def quantise_weights(e):
            wcs[e] = wcp.tile([P, H], U32, tag="wc", name="wc%d" % e, align_bytes=64)
            wss[e] = wcp.tile([P, H], U8, tag="ws", name="ws%d" % e, align_bytes=64)
            nc.vector.quantize_mx(
                out=wcs[e][:].bitcast(FP8X4), scales=wss[e][:], in_=wgs[e][:].rearrange("p h j -> p (h j)")
            )

        gs = cst.tile([P, E, B, PACK], BF16, name="gs", align_bytes=64)
        sc = cst.tile([P, E, B], U32, name="sc", align_bytes=64)
        ss = cst.tile([P, E, B], U8, name="ss", align_bytes=64)

        def quantise_slots(k):
            nc.vector.quantize_mx(
                out=sc[:, 2 * k:2 * k + 2, :].rearrange("p e b -> p (e b)").bitcast(FP8X4),
                scales=ss[:, 2 * k:2 * k + 2, :].rearrange("p e b -> p (e b)"),
                in_=gs[:, 2 * k:2 * k + 2, :, :].rearrange("p e b j -> p (e b j)"),
            )

        accs = {}

        def sum_step(t, n):
            for i in range(NV):
                if n == 0:
                    accs[i] = acp.tile([P, D], F32, tag="acc%d" % i, name="acc%d_%d" % (t, i))
                    nc.vector.tensor_scalar_mul(out=accs[i][:], in0=tns[t][:, 0, :], scalar1=dn[:, t, i, 0:1])
                else:
                    nc.vector.scalar_tensor_tensor(
                        out=accs[i][:], in0=tns[t][:, n, :], scalar=dn[:, t, i, n:n + 1], in1=accs[i][:],
                        op0=ALU.mult, op1=ALU.add,
                    )

        psts = {}

        def sum_transpose(t):
            for i in range(NV):
                psts[i] = psH.tile([P, PACK, P], F32, tag="ph", name="pst%d_%d" % (t, i))
                for j in range(PACK):
                    nc.tensor.transpose(psts[i][:, j, :], accs[i][:, P * j:P * j + P], ident[:])

        def sum_store(t):
            for i in range(NV):
                nc.vector.tensor_copy(out=gs[:, EP + i, P * t:P * t + P, :], in_=psts[i][:].rearrange("p j b -> p b j"))

        for g in range(G):
            ps = psH.tile([P, PACK, EP * GB], F32, tag="ph", name="ps%d" % g)
            for j in range(PACK):
                nc.tensor.matmul(
                    ps[:, j, :],
                    lhsT=tfs[g // 4][:, g % 4, P * j:P * j + P],
                    rhs=dblk[:, g, :, :].rearrange("p e b -> p (e b)"),
                    start=True,
                    stop=True,
                )
            nc.scalar.copy(out=gs[:, 0:EP, GB * g:GB * g + GB, :], in_=ps[:].rearrange("p j (e b) -> p e b j", e=EP))
            if g % 4 == 0:
                regroup(g // 4)
            if g % 4 == 2:
                quantise_weights(g // 4)
            if g % 8 == 4:
                load_bias(g // 8)
            if 4 <= g < 4 + NA:
                sum_step(0, g - 4)
        load_tokens_by_batch(1)
        quantise_slots(0)

        xs, us, negmus, vss, rstds, mvs = {}, {}, {}, {}, {}, {}
        junk = cst.tile([P, H], BF16, name="junk")
        out_v = out.rearrange("(t b) e h -> b t e h", b=P)

        phs = {}

        def multiply(e):
            for t in range(2):
                for hh in range(2):
                    phs[(e, t, hh)] = psH.tile([P, 512], F32, tag="ph", name="ph%d_%d_%d" % (e, t, hh))
                    nc.tensor.matmul_mx(
                        out=phs[(e, t, hh)][:],
                        lhsT=sc[:, e, P * t:P * t + P].bitcast(FP8X4),
                        lhsT_scale=ss[:, e, P * t:P * t + P],
                        rhs=wcs[e][:, 512 * hh:512 * hh + 512].bitcast(FP8X4),
                        rhs_scale=wss[e][:, 512 * hh:512 * hh + 512],
                        start=True,
                        stop=True,
                    )

        def add_bias(e, t):
            by_vector = e // 2 >= VECTOR_STATS_FROM
            if t == 0:
                xs[e] = xp.tile([P, 2, H], F32, tag="x", name="x%d" % e)
            if t == 0 and not by_vector:
                negmus[e] = stp.tile([P, 2], F32, tag="negmu", name="negmu%d" % e)
            if not by_vector:
                s01 = stp.tile([P, 2], F32, tag="s01", name="s01_%d_%d" % (e, t))
            for hh in range(2):
                nc.vector.scalar_tensor_tensor(
                    out=xs[e][:, t, 512 * hh:512 * hh + 512],
                    in0=phs[(e, t, hh)][:],
                    scalar=1.0,
                    in1=bb[:, e, 512 * hh:512 * hh + 512],
                    op0=ALU.mult,
                    op1=ALU.add,
                    accum_out=None if by_vector else s01[:, hh:hh + 1],
                )
            if not by_vector:
                nc.vector.tensor_scalar(
                    out=negmus[e][:, t:t + 1], in0=s01[:, 0:1], scalar1=s01[:, 1:2], scalar2=-1.0 / H,
                    op0=ALU.add, op1=ALU.mult,
                )
            else:
                if e % 2 == 0 and t == 0:
                    mvs[e // 2] = stp.tile([P, 4, 2], F32, tag="mv", name="mv%d" % (e // 2))
                st6 = stp.tile([P, 2, 6], F32, tag="st6", name="st6_%d_%d" % (e, t))
                for hh in range(2):
                    nc.vector.bn_stats(out=st6[:, hh, :], in_=xs[e][:, t, 512 * hh:512 * hh + 512])
                nc.vector.bn_aggr(out=mvs[e // 2][:, 2 * (e % 2) + t, :], in_=st6[:].rearrange("p a s -> p (a s)"))

        def centre_times_gamma(e):
            us[e] = up.tile([P, 2, H], F32, tag="u", name="u%d" % e)
            for t in range(2):
                if e // 2 >= VECTOR_STATS_FROM:
                    nc.vector.scalar_tensor_tensor(
                        out=us[e][:, t, :], in0=xs[e][:, t, :], scalar=mvs[e // 2][:, 2 * (e % 2) + t, 0:1], in1=pgs[e][:],
                        op0=ALU.subtract, op1=ALU.mult,
                    )
                else:
                    nc.vector.scalar_tensor_tensor(
                        out=us[e][:, t, :], in0=xs[e][:, t, :], scalar=negmus[e][:, t:t + 1], in1=pgs[e][:],
                        op0=ALU.add, op1=ALU.mult,
                    )
            if e + 2 < E:
                spread(0, e + 2)

        def sum_of_squares(k, i):
            e = 2 * k + i
            if k >= VECTOR_STATS_FROM:
                return
            if i == 0:
                vss[k] = stp.tile([P, 4], F32, tag="vs", name="vs%d" % k)
            for t in range(2):
                nc.scalar.activation(
                    out=junk[:], in_=xs[e][:, t, :], func=ACT.Square, bias=negmus[e][:, t:t + 1],
                    accum_out=vss[k][:, 2 * i + t:2 * i + t + 1],
                )

        def inverse_deviation(k):
            ve = stp.tile([P, 4], F32, tag="ve", name="ve%d" % k)
            rstds[k] = stp.tile([P, 4], F32, tag="rstd", name="rstd%d" % k)
            if k >= VECTOR_STATS_FROM:
                nc.gpsimd.tensor_scalar(out=ve[:], in0=mvs[k][:, :, 1], scalar1=1.0, scalar2=EPS, op0=ALU.mult, op1=ALU.add)
            else:
                nc.gpsimd.tensor_scalar(out=ve[:], in0=vss[k][:], scalar1=1.0 / H, scalar2=EPS, op0=ALU.mult, op1=ALU.add)
            nc.gpsimd.tensor_tensor(out=rstds[k][:], in0=ve[:], in1=mhalf[:], op=ALU.pow)

        def scale_add_beta(k, i):
            e = 2 * k + i
            for t in range(2):
                nc.vector.scalar_tensor_tensor(
                    out=xs[e][:, t, :], in0=us[e][:, t, :], scalar=rstds[k][:, 2 * i + t:2 * i + t + 1], in1=pbs[e][:],
                    op0=ALU.mult, op1=ALU.add,
                )
            if e + 2 < E:
                spread(1, e + 2)

        def flat(tl):
            return tl[:].rearrange("p t h -> p (t h)")

        def finish(k, i):
            e = 2 * k + i
            eng = nc.gpsimd if k < POOL_BATCHES else nc.vector
            if k < NB - 1:
                nc.scalar.activation(out=flat(us[e]), in_=flat(us[e]), func=ACT.Tanh)
                for t in range(2):
                    eng.tensor_tensor(out=us[e][:, t, :], in0=xs[e][:, t, :], in1=us[e][:, t, :], op=ALU.mult)
                nc.sync.dma_start(out=out_v[:, :, e, :], in_=us[e][:])
            else:
                for t in range(2):
                    nc.scalar.activation(out=us[e][:, t, :], in_=us[e][:, t, :], func=ACT.Tanh)
                    eng.tensor_tensor(out=us[e][:, t, :], in0=xs[e][:, t, :], in1=us[e][:, t, :], op=ALU.mult)
                    nc.sync.dma_start(out=out_v[:, t, e, :], in_=us[e][:, t, :])

        def head(k):
            add_bias(2 * k, 0)
            add_bias(2 * k, 1)
            multiply(2 * k + 1)
            centre_times_gamma(2 * k)
            add_bias(2 * k + 1, 0)
            add_bias(2 * k + 1, 1)
            centre_times_gamma(2 * k + 1)

        multiply(0)
        head(0)
        quantise_slots(1)
        for c in range(-1, NB):
            if c + 2 < NB:
                multiply(2 * (c + 2))
            for i in range(2):
                if c >= 0:
                    nc.scalar.activation(out=flat(us[2 * c + i]), in_=flat(us[2 * c + i]), func=ACT.Ln, bias=1.0)
                if c + 1 < NB:
                    sum_of_squares(c + 1, i)
            if c + 1 < NB:
                inverse_deviation(c + 1)
                for i in range(2):
                    scale_add_beta(c + 1, i)
            if c >= 0:
                for i in range(2):
                    finish(c, i)
            if c + 1 < NB:
                for i in range(2):
                    e = 2 * (c + 1) + i
                    nc.scalar.activation(out=flat(us[e]), in_=flat(xs[e]), func=ACT.Exp)
            if c + 2 < NB:
                head(c + 2)
            if c + 3 < NB:
                if c == -1:
                    sum_transpose(0)
                regroup(2 * (c + 3))
                regroup(2 * (c + 3) + 1)
                if c == -1:
                    quantise_slots(2)
                    sum_store(0)
                for n in range(4 * (c + 1), 4 * (c + 1) + 4):
                    sum_step(1, n)
                if c == 0:
                    sum_transpose(1)
                quantise_weights(2 * (c + 3))
                quantise_weights(2 * (c + 3) + 1)
                if c == 0:
                    sum_store(1)
                    quantise_slots(3)
